import numpy as np
import ml_dtypes


def mxq(x, axis, fmt="e4m3"):
    dtype, down = {"e4m3": (ml_dtypes.float8_e4m3fn, 7), "e5m2": (ml_dtypes.float8_e5m2, 14)}[fmt]
    v = np.moveaxis(np.asarray(x, np.float32).astype(ml_dtypes.bfloat16).astype(np.float64), axis, -1)
    blocks = v.reshape(v.shape[:-1] + (-1, 32))
    amax = np.abs(blocks).max(-1, keepdims=True)
    byte = np.maximum(np.where(amax > 0, np.frexp(amax)[1] - 1 + 127, 0) - down, 1)
    scale = np.exp2(byte - 127.0)
    codes = (blocks / scale).astype(np.float32).astype(dtype).astype(np.float64)
    return np.moveaxis((codes * scale).reshape(v.shape), -1, axis)


WIDE = False


def mx_kscale(k):
    if not WIDE:
        return np.ones(k)
    levels = np.array([10, -10, 5, -5, 0])
    a = np.random.permutation(np.resize(levels, k // 512 * 4)).reshape(k // 512, 4)
    idx = np.arange(k)
    return np.exp2(a[idx // 512, idx % 128 // 32])


BF16 = ml_dtypes.bfloat16


def bf(x):
    return np.asarray(x, np.float32).astype(BF16)


def f64(x):
    return np.asarray(x).astype(np.float64)


B, SQ, SKV, DIN, Q_HEADS, KV_HEADS, DIMS = 2, 512, 512, 2048, 16, 4, 2048
HEAD_DIM = DIMS // Q_HEADS
REP = Q_HEADS // KV_HEADS


def setup_inputs():
    s = mx_kscale(DIN)
    return {
        "xq": bf(np.random.standard_normal((B, SQ, DIMS)) * 2.0),
        "xk_rep": bf(np.repeat(np.random.standard_normal((B, SKV, KV_HEADS * HEAD_DIM)) * 1.5, REP, axis=-1)),
        "kv": bf(np.random.standard_normal((B, SKV, DIN)) * s),
        "mask": bf(np.random.uniform(0.25, 1.0, (1, 1, SQ, SKV))),
        "Wv": bf(np.random.standard_normal((DIN, KV_HEADS * HEAD_DIM)) / np.sqrt(DIN) / s[:, None]),
    }


def reference(xq, xk_rep, kv, mask, Wv):
    xv = mxq(f64(kv), 2, "e4m3") @ mxq(f64(Wv), 0, "e4m3")
    xv = np.repeat(xv, REP, axis=-1)
    qh = f64(xq).reshape(B, SQ, Q_HEADS, HEAD_DIM).transpose(0, 2, 1, 3)
    kh = f64(xk_rep).reshape(B, SKV, Q_HEADS, HEAD_DIM).transpose(0, 2, 3, 1)
    vh = xv.reshape(B, SKV, Q_HEADS, HEAD_DIM).transpose(0, 2, 1, 3)
    scores = (qh @ kh) * (HEAD_DIM ** -0.5)
    scores = scores - (1.0 / f64(mask) - 1.0)
    e = np.exp(scores - scores.max(-1, keepdims=True))
    out = (mxq(e, 3, "e4m3") @ mxq(vh, 2, "e4m3")) / e.sum(-1, keepdims=True)
    return out.transpose(0, 2, 1, 3).reshape(B, SQ, DIMS)

@@ -1,0 +1,280 @@
+from contextlib import ExitStack
+
+import concourse.mybir as mybir
+from concourse.masks import make_identity
+
+F32 = mybir.dt.float32
+BF16 = mybir.dt.bfloat16
+U32 = mybir.dt.uint32
+U8 = mybir.dt.uint8
+FP8X4 = mybir.dt.float8_e4m3fn_x4
+ALU = mybir.AluOpType
+ACT = mybir.ActivationFunctionType
+AXIS = mybir.AxisListType
+
+P = 128
+PACK = 4
+K_PASS = P * PACK
+
+B, SQ, SKV, DIN, HEADS, DIMS = 2, 512, 512, 2048, 16, 2048
+HEAD_DIM = DIMS // HEADS
+XV = 512
+REP = 4
+OWN = HEAD_DIM // REP
+GROUP = 4
+N_GROUPS = HEADS // GROUP
+Q_TILES = SQ // P
+KEY_TILES = SKV // P
+PASSES = DIN // K_PASS
+SCALE = HEAD_DIM ** -0.5
+
+FLOPS = 2 * B * SKV * DIN * XV + 2 * 2 * B * HEADS * SQ * SKV * HEAD_DIM
+
+
+def tile_groupedqueryattention_pa_kernel(tc, xq, xk_rep, kv, mask, Wv, out):
+    nc = tc.nc
+    xq_rows = xq.flatten_outer_dims()
+    xk_rows = xk_rep.flatten_outer_dims()
+    kv_rows = kv.flatten_outer_dims()
+    out_rows = out.flatten_outer_dims()
+    mask_rows = mask.rearrange("a b q k -> (a b q) k")
+
+    with ExitStack() as ctx:
+        const = ctx.enter_context(tc.tile_pool(name="const", bufs=1))
+        raw = ctx.enter_context(tc.tile_pool(name="raw", bufs=4))
+        stage = ctx.enter_context(tc.tile_pool(name="stage", bufs=2))
+        keep = ctx.enter_context(tc.tile_pool(name="keep", bufs=1))
+        work = ctx.enter_context(tc.tile_pool(name="work", bufs=2))
+        psum_s = ctx.enter_context(tc.psum_pool(name="psum_s", bufs=3))
+        psum_t = ctx.enter_context(tc.psum_pool(name="psum_t", bufs=3))
+        psum_o = ctx.enter_context(tc.psum_pool(name="psum_o", bufs=2))
+
+        ident_bf = const.tile([P, P], BF16)
+        make_identity(nc, ident_bf[:])
+        ident_f32 = const.tile([P, P], F32)
+        make_identity(nc, ident_f32[:])
+
+        mask_sb = const.tile([P, Q_TILES, SKV], BF16)
+        nc.sync.dma_start(out=mask_sb[:], in_=mask_rows.rearrange("(t p) k -> p t k", p=P))
+        penalty = const.tile([P, Q_TILES, SKV], F32)
+
+        def make_penalty(qt):
+            nc.vector.reciprocal(out=penalty[:, qt, :], in_=mask_sb[:, qt, :])
+            nc.vector.tensor_scalar_add(
+                out=penalty[:, qt, :], in0=penalty[:, qt, :], scalar1=-1.0
+            )
+
+        wv_codes = const.tile([P, PASSES, XV], U32, align_bytes=64)
+        wv_scales = const.tile([P, PASSES, XV], U8, align_bytes=64)
+        wv_view = Wv.rearrange("(g u p e) c -> g p u (e c)", g=PASSES, u=2, p=P, e=2)
+        for g in range(PASSES):
+            wv_raw = stage.tile([P, 2, 2 * XV], BF16)
+            nc.sync.dma_start(out=wv_raw[:], in_=wv_view[g])
+            wv_grouped = stage.tile([P, XV, PACK], BF16, align_bytes=64)
+            nc.vector.tensor_copy(
+                out=wv_grouped[:].rearrange("p (c i) t -> p c t i", i=4),
+                in_=wv_raw[:]
+                .rearrange("p u (e c) -> p (u e) c", e=2)
+                .rearrange("p t (c i) -> p c t i", i=4),
+            )
+            nc.vector.quantize_mx(
+                out=wv_codes[:, g, :].bitcast(FP8X4),
+                scales=wv_scales[:, g, :],
+                in_=wv_grouped[:].rearrange("p c t -> p (c t)"),
+            )
+
+        def project_values(b):
+            kv_codes = keep.tile([P, KEY_TILES, PASSES, P], U32, align_bytes=64)
+            kv_scales = keep.tile([P, KEY_TILES, PASSES, P], U8, align_bytes=64)
+            for t in range(KEY_TILES):
+                kv_raw = raw.tile([P, DIN], BF16)
+                first = b * SKV + t * P
+                nc.sync.dma_start(out=kv_raw[:], in_=kv_rows[first : first + P, :])
+                kv_words = kv_raw[:].bitcast(F32)
+                kv_grouped = stage.tile([P, PASSES * P * PACK], BF16, align_bytes=64)
+                grouped_words = kv_grouped[:].bitcast(F32).rearrange(
+                    "p (g r u) -> p g r u", g=PASSES, r=P
+                )
+                for half in range(PASSES // 2):
+                    kvT_ps = psum_t.tile([P, 2, 2, P], F32, tag="t")
+                    for a in range(2):
+                        for u in range(2):
+                            w0 = (2 * half + a) * (K_PASS // 2) + u * P
+                            nc.tensor.transpose(
+                                kvT_ps[:, a, u, :], kv_words[:, w0 : w0 + P], ident_f32[:]
+                            )
+                    nc.scalar.copy(
+                        out=grouped_words[:, 2 * half : 2 * half + 2, :, :],
+                        in_=kvT_ps[:].rearrange("p a u r -> p a r u"),
+                    )
+                nc.vector.quantize_mx(
+                    out=kv_codes[:, t].rearrange("p g r -> p (g r)").bitcast(FP8X4),
+                    scales=kv_scales[:, t].rearrange("p g r -> p (g r)"),
+                    in_=kv_grouped[:],
+                )
+
+            v_grouped = stage.tile([P, XV, PACK], BF16, align_bytes=64)
+            for j in range(XV // P):
+                cols = slice(j * P, (j + 1) * P)
+                xv_ps = psum_s.tile([P, KEY_TILES, P], F32, tag="s")
+                for t in range(KEY_TILES):
+                    for g in range(PASSES):
+                        nc.tensor.matmul_mx(
+                            out=xv_ps[:, t, :],
+                            lhsT=kv_codes[:, t, g, :].bitcast(FP8X4),
+                            lhsT_scale=kv_scales[:, t, g, :],
+                            rhs=wv_codes[:, g, cols].bitcast(FP8X4),
+                            rhs_scale=wv_scales[:, g, cols],
+                            start=(g == 0),
+                            stop=(g == PASSES - 1),
+                        )
+                nc.scalar.copy(
+                    out=v_grouped[:, cols, :], in_=xv_ps[:].rearrange("p t f -> p f t")
+                )
+            v_codes = keep.tile([P, XV], U32, align_bytes=64, tag="v_codes", bufs=B)
+            v_scales = keep.tile([P, XV], U8, align_bytes=64, tag="v_scales", bufs=B)
+            nc.vector.quantize_mx(
+                out=v_codes[:].bitcast(FP8X4),
+                scales=v_scales[:],
+                in_=v_grouped[:].rearrange("p f t -> p (f t)"),
+            )
+            return v_codes, v_scales
+
+        values = [project_values(b) for b in range(B)]
+
+        for b in range(B):
+            v_codes, v_scales = values[b]
+
+            xk_raw = []
+            for kt in range(KEY_TILES):
+                xk_tile = raw.tile([P, DIMS], BF16, tag="xk_raw", name="xk_tile")
+                first = b * SKV + kt * P
+                nc.sync.dma_start(out=xk_tile[:], in_=xk_rows[first : first + P, :])
+                xk_raw.append(xk_tile)
+            kT = [None] * N_GROUPS
+
+            for qt in range(Q_TILES):
+                if b == 0:
+                    make_penalty(qt)
+
+                xq_raw = raw.tile([P, DIMS], BF16)
+                first = b * SQ + qt * P
+                nc.sync.dma_start(out=xq_raw[:], in_=xq_rows[first : first + P, :])
+                qT = work.tile([P, HEADS, P], BF16)
+                for half in range(2):
+                    qT_ps = psum_t.tile([P, 8, P], BF16, tag="t")
+                    for a in range(8):
+                        h = 8 * half + a
+                        nc.tensor.transpose(
+                            qT_ps[:, a, :], xq_raw[:, h * P : (h + 1) * P], ident_bf[:]
+                        )
+                    nc.scalar.copy(out=qT[:, 8 * half : 8 * half + 8, :], in_=qT_ps[:])
+
+                for hg in range(N_GROUPS):
+                    if qt == 0:
+                        kT[hg] = keep.tile(
+                            [P, GROUP, SKV], BF16, tag="kT%d" % hg, name="kT%d" % hg
+                        )
+                        for half in range(2):
+                            kT_ps = psum_t.tile([P, 2, KEY_TILES, P], BF16, tag="t")
+                            for a in range(2):
+                                h = GROUP * hg + 2 * half + a
+                                for kt in range(KEY_TILES):
+                                    nc.tensor.transpose(
+                                        kT_ps[:, a, kt, :],
+                                        xk_raw[kt][:, h * P : (h + 1) * P],
+                                        ident_bf[:],
+                                    )
+                            nc.scalar.copy(
+                                out=kT[hg][:, 2 * half : 2 * half + 2, :],
+                                in_=kT_ps[:].rearrange("p a k r -> p a (k r)"),
+                            )
+
+                    s_sb = work.tile([P, GROUP, SKV], F32)
+                    for hh in range(GROUP):
+                        s_ps = psum_s.tile([P, SKV], F32, tag="s")
+                        nc.tensor.matmul(
+                            out=s_ps[:],
+                            lhsT=qT[:, GROUP * hg + hh, :],
+                            rhs=kT[hg][:, hh, :],
+                            start=True,
+                            stop=True,
+                        )
+                        nc.vector.scalar_tensor_tensor(
+                            out=s_sb[:, hh, :],
+                            in0=s_ps[:],
+                            scalar=SCALE,
+                            in1=penalty[:, qt, :],
+                            op0=ALU.mult,
+                            op1=ALU.subtract,
+                        )
+                    neg_max = work.tile([P, GROUP], F32)
+                    nc.vector.tensor_reduce(
+                        out=neg_max[:], in_=s_sb[:], axis=AXIS.X, op=ALU.max, negate=True
+                    )
+
+                    e_sb = work.tile([P, GROUP, SKV], BF16)
+                    row_sum = work.tile([P, GROUP], F32)
+                    for hh in range(GROUP):
+                        nc.scalar.activation(
+                            out=e_sb[:, hh, :],
+                            in_=s_sb[:, hh, :],
+                            func=ACT.Exp,
+                            bias=neg_max[:, hh : hh + 1],
+                            scale=1.0,
+                            accum_out=row_sum[:, hh : hh + 1],
+                        )
+                    inv_sum = work.tile([P, GROUP], F32)
+                    nc.vector.reciprocal(out=inv_sum[:], in_=row_sum[:])
+
+                    e_grouped = work.tile([P, GROUP, P, PACK], BF16, align_bytes=64)
+                    for half in range(2):
+                        eT_ps = psum_t.tile([P, 2, KEY_TILES, P], BF16, tag="t")
+                        for a in range(2):
+                            for t in range(KEY_TILES):
+                                nc.tensor.transpose(
+                                    eT_ps[:, a, t, :],
+                                    e_sb[:, 2 * half + a, t * P : (t + 1) * P],
+                                    ident_bf[:],
+                                )
+                        nc.scalar.copy(
+                            out=e_grouped[:, 2 * half : 2 * half + 2, :, :],
+                            in_=eT_ps[:].rearrange("p a t q -> p a q t"),
+                        )
+                    e_codes = work.tile([P, GROUP * P], U32, align_bytes=64)
+                    e_scales = work.tile([P, GROUP * P], U8, align_bytes=64)
+                    nc.vector.quantize_mx(
+                        out=e_codes[:].bitcast(FP8X4),
+                        scales=e_scales[:],
+                        in_=e_grouped[:].rearrange("p h q t -> p (h q t)"),
+                    )
+
+                    o_ps = psum_o.tile([P, GROUP, GROUP * OWN], F32)
+                    group_cols = slice(hg * P, (hg + 1) * P)
+                    for hh in range(GROUP):
+                        queries = slice(hh * P, (hh + 1) * P)
+                        nc.tensor.matmul_mx(
+                            out=o_ps[:, hh, :],
+                            lhsT=e_codes[:, queries].bitcast(FP8X4),
+                            lhsT_scale=e_scales[:, queries],
+                            rhs=v_codes[:, group_cols].bitcast(FP8X4),
+                            rhs_scale=v_scales[:, group_cols],
+                            start=True,
+                            stop=True,
+                        )
+                    own = o_ps[:].rearrange("p h (g c) -> p (h g) c", c=OWN)[
+                        :, 0 : GROUP * GROUP : GROUP + 1, :
+                    ]
+                    shape = [P, GROUP, OWN, REP]
+                    o_sb = work.tile(shape, F32, bufs=3)
+                    nc.vector.tensor_tensor(
+                        out=o_sb[:],
+                        in0=own.unsqueeze(3).to_broadcast(shape),
+                        in1=inv_sum[:].unsqueeze(2).unsqueeze(3).to_broadcast(shape),
+                        op=ALU.mult,
+                    )
+                    first = b * SQ + qt * P
+                    nc.gpsimd.dma_start(
+                        out=out_rows[first : first + P, hg * GROUP * P : (hg + 1) * GROUP * P],
+                        in_=o_sb[:].rearrange("p h c r -> p (h c r)"),
+                    )

@@ -21,12 +21,22 @@ HEAD_DIM = DIMS // HEADS
 XV = 512
 REP = 4
 OWN = HEAD_DIM // REP
-GROUP = 4
+GROUP = P // OWN
 N_GROUPS = HEADS // GROUP
 Q_TILES = SQ // P
 KEY_TILES = SKV // P
 PASSES = DIN // K_PASS
 SCALE = HEAD_DIM ** -0.5
+
+PAIR = 2
+PAIRS = HEADS // PAIR
+N_ITEMS = B * Q_TILES * PAIRS
+LAG_EXP = 1
+LAG_TRANSPOSE = 2
+LAG_REGROUP = 3
+LAG_QUANTISE = 4
+LAG_OUT = 5
+VECTOR_SHARE = 4
 
 FLOPS = 2 * B * SKV * DIN * XV + 2 * 2 * B * HEADS * SQ * SKV * HEAD_DIM
 
@@ -44,10 +54,10 @@ def tile_groupedqueryattention_pa_kernel(tc, xq, xk_rep, kv, mask, Wv, out):
         raw = ctx.enter_context(tc.tile_pool(name="raw", bufs=4))
         stage = ctx.enter_context(tc.tile_pool(name="stage", bufs=2))
         keep = ctx.enter_context(tc.tile_pool(name="keep", bufs=1))
-        work = ctx.enter_context(tc.tile_pool(name="work", bufs=2))
-        psum_s = ctx.enter_context(tc.psum_pool(name="psum_s", bufs=3))
+        work = ctx.enter_context(tc.tile_pool(name="work", bufs=3))
+        psum_s = ctx.enter_context(tc.psum_pool(name="psum_s", bufs=4))
         psum_t = ctx.enter_context(tc.psum_pool(name="psum_t", bufs=3))
-        psum_o = ctx.enter_context(tc.psum_pool(name="psum_o", bufs=2))
+        psum_o = ctx.enter_context(tc.psum_pool(name="psum_o", bufs=1))
 
         ident_bf = const.tile([P, P], BF16)
         make_identity(nc, ident_bf[:])
@@ -57,12 +67,19 @@ def tile_groupedqueryattention_pa_kernel(tc, xq, xk_rep, kv, mask, Wv, out):
         mask_sb = const.tile([P, Q_TILES, SKV], BF16)
         nc.sync.dma_start(out=mask_sb[:], in_=mask_rows.rearrange("(t p) k -> p t k", p=P))
         penalty = const.tile([P, Q_TILES, SKV], F32)
-
-        def make_penalty(qt):
+        neg_penT = const.tile([P, KEY_TILES, SQ], F32)
+        for qt in range(Q_TILES):
+            queries = slice(qt * P, (qt + 1) * P)
             nc.vector.reciprocal(out=penalty[:, qt, :], in_=mask_sb[:, qt, :])
             nc.vector.tensor_scalar_add(
                 out=penalty[:, qt, :], in0=penalty[:, qt, :], scalar1=-1.0
             )
+            pT_ps = psum_t.tile([P, KEY_TILES, P], F32, tag="t")
+            for kt in range(KEY_TILES):
+                nc.tensor.transpose(
+                    pT_ps[:, kt, :], penalty[:, qt, kt * P : (kt + 1) * P], ident_f32[:]
+                )
+            nc.scalar.mul(out=neg_penT[:, :, queries], in_=pT_ps[:], mul=-1.0 / SCALE)
 
         wv_codes = const.tile([P, PASSES, XV], U32, align_bytes=64)
         wv_scales = const.tile([P, PASSES, XV], U8, align_bytes=64)
@@ -142,139 +159,189 @@ def tile_groupedqueryattention_pa_kernel(tc, xq, xk_rep, kv, mask, Wv, out):
 
         values = [project_values(b) for b in range(B)]
 
+        xk_raw = {}
+        xq_raw = {}
         for b in range(B):
-            v_codes, v_scales = values[b]
-
-            xk_raw = []
             for kt in range(KEY_TILES):
-                xk_tile = raw.tile([P, DIMS], BF16, tag="xk_raw", name="xk_tile")
+                xk_tile = raw.tile([P, DIMS], BF16, tag="xk", bufs=B * KEY_TILES)
                 first = b * SKV + kt * P
                 nc.sync.dma_start(out=xk_tile[:], in_=xk_rows[first : first + P, :])
-                xk_raw.append(xk_tile)
-            kT = [None] * N_GROUPS
-
+                xk_raw[(b, kt)] = xk_tile
             for qt in range(Q_TILES):
-                if b == 0:
-                    make_penalty(qt)
-
-                xq_raw = raw.tile([P, DIMS], BF16)
+                xq_tile = raw.tile([P, DIMS], BF16, tag="xq", bufs=B * Q_TILES)
                 first = b * SQ + qt * P
-                nc.sync.dma_start(out=xq_raw[:], in_=xq_rows[first : first + P, :])
-                qT = work.tile([P, HEADS, P], BF16)
+                nc.sync.dma_start(out=xq_tile[:], in_=xq_rows[first : first + P, :])
+                xq_raw[(b, qt)] = xq_tile
+
+        qT_of, kT_of = {}, {}
+        scores_of, shift_of, e_of, sum_of, eT_of = {}, {}, {}, {}, {}
+        grouped_of, codes_of, inv_sum_of, o_of = {}, {}, {}, {}
+
+        def where(n):
+            b, rest = divmod(n, Q_TILES * PAIRS)
+            qt, pair = divmod(rest, PAIRS)
+            return b, qt, pair
+
+        def prepare(n):
+            b, qt, pair = where(n)
+            if pair == 0:
+                qT = work.tile([P, HEADS, P], BF16, bufs=2)
                 for half in range(2):
-                    qT_ps = psum_t.tile([P, 8, P], BF16, tag="t")
-                    for a in range(8):
-                        h = 8 * half + a
+                    qT_ps = psum_t.tile([P, HEADS // 2, P], BF16, tag="t")
+                    for a in range(HEADS // 2):
+                        h = half * (HEADS // 2) + a
                         nc.tensor.transpose(
-                            qT_ps[:, a, :], xq_raw[:, h * P : (h + 1) * P], ident_bf[:]
+                            qT_ps[:, a, :], xq_raw[(b, qt)][:, h * P : (h + 1) * P], ident_bf[:]
                         )
-                    nc.scalar.copy(out=qT[:, 8 * half : 8 * half + 8, :], in_=qT_ps[:])
-
-                for hg in range(N_GROUPS):
-                    if qt == 0:
-                        kT[hg] = keep.tile(
-                            [P, GROUP, SKV], BF16, tag="kT%d" % hg, name="kT%d" % hg
-                        )
-                        for half in range(2):
-                            kT_ps = psum_t.tile([P, 2, KEY_TILES, P], BF16, tag="t")
-                            for a in range(2):
-                                h = GROUP * hg + 2 * half + a
-                                for kt in range(KEY_TILES):
-                                    nc.tensor.transpose(
-                                        kT_ps[:, a, kt, :],
-                                        xk_raw[kt][:, h * P : (h + 1) * P],
-                                        ident_bf[:],
-                                    )
-                            nc.scalar.copy(
-                                out=kT[hg][:, 2 * half : 2 * half + 2, :],
-                                in_=kT_ps[:].rearrange("p a k r -> p a (k r)"),
-                            )
-
-                    s_sb = work.tile([P, GROUP, SKV], F32)
-                    for hh in range(GROUP):
-                        s_ps = psum_s.tile([P, SKV], F32, tag="s")
-                        nc.tensor.matmul(
-                            out=s_ps[:],
-                            lhsT=qT[:, GROUP * hg + hh, :],
-                            rhs=kT[hg][:, hh, :],
-                            start=True,
-                            stop=True,
-                        )
-                        nc.vector.scalar_tensor_tensor(
-                            out=s_sb[:, hh, :],
-                            in0=s_ps[:],
-                            scalar=SCALE,
-                            in1=penalty[:, qt, :],
-                            op0=ALU.mult,
-                            op1=ALU.subtract,
-                        )
-                    neg_max = work.tile([P, GROUP], F32)
-                    nc.vector.tensor_reduce(
-                        out=neg_max[:], in_=s_sb[:], axis=AXIS.X, op=ALU.max, negate=True
+                    nc.scalar.copy(
+                        out=qT[:, half * (HEADS // 2) : (half + 1) * (HEADS // 2), :],
+                        in_=qT_ps[:],
                     )
-
-                    e_sb = work.tile([P, GROUP, SKV], BF16)
-                    row_sum = work.tile([P, GROUP], F32)
-                    for hh in range(GROUP):
-                        nc.scalar.activation(
-                            out=e_sb[:, hh, :],
-                            in_=s_sb[:, hh, :],
-                            func=ACT.Exp,
-                            bias=neg_max[:, hh : hh + 1],
-                            scale=1.0,
-                            accum_out=row_sum[:, hh : hh + 1],
+                qT_of[(b, qt)] = qT
+            if qt == 0:
+                kT = keep.tile([P, PAIR, SKV], BF16, tag="kT%d" % pair)
+                kT_ps = psum_t.tile([P, PAIR, KEY_TILES, P], BF16, tag="t")
+                for a in range(PAIR):
+                    h = PAIR * pair + a
+                    for kt in range(KEY_TILES):
+                        nc.tensor.transpose(
+                            kT_ps[:, a, kt, :],
+                            xk_raw[(b, kt)][:, h * P : (h + 1) * P],
+                            ident_bf[:],
                         )
-                    inv_sum = work.tile([P, GROUP], F32)
-                    nc.vector.reciprocal(out=inv_sum[:], in_=row_sum[:])
+                nc.scalar.copy(out=kT[:], in_=kT_ps[:].rearrange("p a k r -> p a (k r)"))
+                kT_of[(b, pair)] = kT
 
-                    e_grouped = work.tile([P, GROUP, P, PACK], BF16, align_bytes=64)
-                    for half in range(2):
-                        eT_ps = psum_t.tile([P, 2, KEY_TILES, P], BF16, tag="t")
-                        for a in range(2):
-                            for t in range(KEY_TILES):
-                                nc.tensor.transpose(
-                                    eT_ps[:, a, t, :],
-                                    e_sb[:, 2 * half + a, t * P : (t + 1) * P],
-                                    ident_bf[:],
-                                )
-                        nc.scalar.copy(
-                            out=e_grouped[:, 2 * half : 2 * half + 2, :, :],
-                            in_=eT_ps[:].rearrange("p a t q -> p a q t"),
-                        )
-                    e_codes = work.tile([P, GROUP * P], U32, align_bytes=64)
-                    e_scales = work.tile([P, GROUP * P], U8, align_bytes=64)
-                    nc.vector.quantize_mx(
-                        out=e_codes[:].bitcast(FP8X4),
-                        scales=e_scales[:],
-                        in_=e_grouped[:].rearrange("p h q t -> p (h q t)"),
+        def scores(n):
+            b, qt, pair = where(n)
+            queries = slice(qt * P, (qt + 1) * P)
+            neg_max = work.tile([P, PAIR], F32)
+            banks = []
+            for a in range(PAIR):
+                s_ps = psum_s.tile([P, SKV], F32, tag="s")
+                nc.tensor.matmul(
+                    out=s_ps[:],
+                    lhsT=qT_of[(b, qt)][:, PAIR * pair + a, :],
+                    rhs=kT_of[(b, pair)][:, a, :],
+                    start=True,
+                    stop=False,
+                )
+                for kt in range(KEY_TILES):
+                    nc.tensor.matmul(
+                        out=s_ps[:, kt * P : (kt + 1) * P],
+                        lhsT=neg_penT[:, kt, queries],
+                        rhs=ident_f32[:],
+                        is_transpose=True,
+                        start=False,
+                        stop=(kt == KEY_TILES - 1),
                     )
+                nc.vector.tensor_reduce(
+                    out=neg_max[:, a : a + 1], in_=s_ps[:], axis=AXIS.X, op=ALU.max, negate=True
+                )
+                banks.append(s_ps)
+            shift = work.tile([P, PAIR], F32)
+            nc.vector.tensor_scalar_mul(out=shift[:], in0=neg_max[:], scalar1=SCALE)
+            scores_of[n] = banks
+            shift_of[n] = shift
 
-                    o_ps = psum_o.tile([P, GROUP, GROUP * OWN], F32)
-                    group_cols = slice(hg * P, (hg + 1) * P)
-                    for hh in range(GROUP):
-                        queries = slice(hh * P, (hh + 1) * P)
-                        nc.tensor.matmul_mx(
-                            out=o_ps[:, hh, :],
-                            lhsT=e_codes[:, queries].bitcast(FP8X4),
-                            lhsT_scale=e_scales[:, queries],
-                            rhs=v_codes[:, group_cols].bitcast(FP8X4),
-                            rhs_scale=v_scales[:, group_cols],
-                            start=True,
-                            stop=True,
-                        )
-                    own = o_ps[:].rearrange("p h (g c) -> p (h g) c", c=OWN)[
-                        :, 0 : GROUP * GROUP : GROUP + 1, :
-                    ]
-                    shape = [P, GROUP, OWN, REP]
-                    o_sb = work.tile(shape, F32, bufs=3)
-                    nc.vector.tensor_tensor(
-                        out=o_sb[:],
-                        in0=own.unsqueeze(3).to_broadcast(shape),
-                        in1=inv_sum[:].unsqueeze(2).unsqueeze(3).to_broadcast(shape),
-                        op=ALU.mult,
+        def exponentials(n):
+            e_sb = work.tile([P, PAIR, SKV], BF16)
+            row_sum = work.tile([P, PAIR], F32, bufs=LAG_QUANTISE - LAG_EXP + 2)
+            for a in range(PAIR):
+                nc.scalar.activation(
+                    out=e_sb[:, a, :],
+                    in_=scores_of[n][a][:],
+                    func=ACT.Exp,
+                    bias=shift_of[n][:, a : a + 1],
+                    scale=SCALE,
+                    accum_out=row_sum[:, a : a + 1],
+                )
+            e_of[n] = e_sb
+            sum_of[n] = row_sum
+
+        def transposes(n):
+            eT_ps = psum_t.tile([P, PAIR, KEY_TILES, P], BF16, tag="t")
+            for a in range(PAIR):
+                for t in range(KEY_TILES):
+                    nc.tensor.transpose(
+                        eT_ps[:, a, t, :], e_of[n][:, a, t * P : (t + 1) * P], ident_bf[:]
                     )
-                    first = b * SQ + qt * P
-                    nc.gpsimd.dma_start(
-                        out=out_rows[first : first + P, hg * GROUP * P : (hg + 1) * GROUP * P],
-                        in_=o_sb[:].rearrange("p h c r -> p (h c r)"),
-                    )
+            eT_of[n] = eT_ps
+
+        def regroup(n):
+            e_grouped = work.tile([P, PAIR, P, PACK], BF16, align_bytes=64)
+            by_word = eT_of[n][:].rearrange("p a t q -> p a q t")
+            if n % VECTOR_SHARE == VECTOR_SHARE - 1:
+                nc.vector.tensor_copy(out=e_grouped[:], in_=by_word)
+            else:
+                nc.scalar.copy(out=e_grouped[:], in_=by_word)
+            grouped_of[n] = e_grouped
+
+        def quantise(n):
+            e_codes = work.tile([P, PAIR * P], U32, align_bytes=64)
+            e_scales = work.tile([P, PAIR * P], U8, align_bytes=64)
+            nc.vector.quantize_mx(
+                out=e_codes[:].bitcast(FP8X4),
+                scales=e_scales[:],
+                in_=grouped_of[n][:].rearrange("p a q t -> p (a q t)"),
+            )
+            inv_sum = work.tile([P, PAIR], F32)
+            nc.vector.reciprocal(out=inv_sum[:], in_=sum_of[n][:])
+            codes_of[n] = (e_codes, e_scales)
+            inv_sum_of[n] = inv_sum
+
+        def multiply(n):
+            b, qt, pair = where(n)
+            e_codes, e_scales = codes_of[n]
+            v_codes, v_scales = values[b]
+            hg = PAIR * pair // GROUP
+            group_cols = slice(hg * P, (hg + 1) * P)
+            o_ps = psum_o.tile([P, PAIR, GROUP * OWN], F32)
+            for a in range(PAIR):
+                queries = slice(a * P, (a + 1) * P)
+                nc.tensor.matmul_mx(
+                    out=o_ps[:, a, :],
+                    lhsT=e_codes[:, queries].bitcast(FP8X4),
+                    lhsT_scale=e_scales[:, queries],
+                    rhs=v_codes[:, group_cols].bitcast(FP8X4),
+                    rhs_scale=v_scales[:, group_cols],
+                    start=True,
+                    stop=True,
+                )
+            o_of[n] = o_ps
+
+        def finish(n):
+            b, qt, pair = where(n)
+            first_own = PAIR * pair % GROUP
+            own = o_of[n][:].rearrange("p a (g c) -> p (a g) c", c=OWN)[
+                :, first_own : first_own + GROUP + 2 : GROUP + 1, :
+            ]
+            shape = [P, PAIR, OWN, REP]
+            o_sb = work.tile(shape, F32, bufs=4)
+            nc.vector.tensor_tensor(
+                out=o_sb[:],
+                in0=own.unsqueeze(3).to_broadcast(shape),
+                in1=inv_sum_of[n][:].unsqueeze(2).unsqueeze(3).to_broadcast(shape),
+                op=ALU.mult,
+            )
+            first = b * SQ + qt * P
+            nc.gpsimd.dma_start(
+                out=out_rows[first : first + P, pair * PAIR * P : (pair + 1) * PAIR * P],
+                in_=o_sb[:].rearrange("p a c r -> p (a c r)"),
+            )
+
+        def at(stage_of_item, n):
+            if 0 <= n < N_ITEMS:
+                stage_of_item(n)
+
+        prepare(0)
+        with tc.manual_schedule():
+            for k in range(N_ITEMS + LAG_OUT):
+                at(regroup, k - LAG_REGROUP)
+                at(quantise, k - LAG_QUANTISE)
+                at(finish, k - LAG_OUT)
+                at(scores, k)
+                at(exponentials, k - LAG_EXP)
+                at(transposes, k - LAG_TRANSPOSE)
+                at(multiply, k - LAG_QUANTISE)
+                at(prepare, k + 1)

@@ -36,7 +36,8 @@ LAG_TRANSPOSE = 2
 LAG_REGROUP = 3
 LAG_QUANTISE = 4
 LAG_OUT = 5
-VECTOR_SHARE = 4
+VECTOR_SHARE = 3
+WAITING = 6
 
 FLOPS = 2 * B * SKV * DIN * XV + 2 * 2 * B * HEADS * SQ * SKV * HEAD_DIM
 
@@ -51,7 +52,7 @@ def tile_groupedqueryattention_pa_kernel(tc, xq, xk_rep, kv, mask, Wv, out):
 
     with ExitStack() as ctx:
         const = ctx.enter_context(tc.tile_pool(name="const", bufs=1))
-        raw = ctx.enter_context(tc.tile_pool(name="raw", bufs=4))
+        raw = ctx.enter_context(tc.tile_pool(name="raw", bufs=B * KEY_TILES))
         stage = ctx.enter_context(tc.tile_pool(name="stage", bufs=2))
         keep = ctx.enter_context(tc.tile_pool(name="keep", bufs=1))
         work = ctx.enter_context(tc.tile_pool(name="work", bufs=3))
@@ -64,33 +65,60 @@ def tile_groupedqueryattention_pa_kernel(tc, xq, xk_rep, kv, mask, Wv, out):
         ident_f32 = const.tile([P, P], F32)
         make_identity(nc, ident_f32[:])
 
+        def load_rows(rows, b, t, tag):
+            tile_sb = raw.tile([P, DIMS], BF16, tag=tag, name=tag)
+            first = (b * KEY_TILES + t) * P
+            nc.sync.dma_start(out=tile_sb[:], in_=rows[first : first + P, :])
+            return tile_sb
+
+        xk_raw, xq_raw, kv_raw = {}, {}, {}
         mask_sb = const.tile([P, Q_TILES, SKV], BF16)
         nc.sync.dma_start(out=mask_sb[:], in_=mask_rows.rearrange("(t p) k -> p t k", p=P))
-        penalty = const.tile([P, Q_TILES, SKV], F32)
-        neg_penT = const.tile([P, KEY_TILES, SQ], F32)
+        for kt in range(KEY_TILES):
+            xk_raw[(0, kt)] = load_rows(xk_rows, 0, kt, "xk")
+        xq_raw[(0, 0)] = load_rows(xq_rows, 0, 0, "xq")
+        wv_raw = const.tile([P, PASSES, 2, 2 * XV], BF16)
+        wv_view = Wv.rearrange("(g u p e) c -> g p u (e c)", g=PASSES, u=2, p=P, e=2)
+        for g in range(PASSES):
+            nc.sync.dma_start(out=wv_raw[:, g], in_=wv_view[g])
+        for t in range(KEY_TILES):
+            kv_raw[(0, t)] = load_rows(kv_rows, 0, t, "kv")
+        for qt in range(1, Q_TILES):
+            xq_raw[(0, qt)] = load_rows(xq_rows, 0, qt, "xq")
+        for t in range(KEY_TILES):
+            kv_raw[(1, t)] = load_rows(kv_rows, 1, t, "kv")
+        for kt in range(KEY_TILES):
+            xk_raw[(1, kt)] = load_rows(xk_rows, 1, kt, "xk")
         for qt in range(Q_TILES):
-            queries = slice(qt * P, (qt + 1) * P)
-            nc.vector.reciprocal(out=penalty[:, qt, :], in_=mask_sb[:, qt, :])
-            nc.vector.tensor_scalar_add(
-                out=penalty[:, qt, :], in0=penalty[:, qt, :], scalar1=-1.0
+            xq_raw[(1, qt)] = load_rows(xq_rows, 1, qt, "xq")
+
+        neg_penT = const.tile([P, KEY_TILES, SQ], F32)
+
+        def penalty_block(qt, kt):
+            pen = work.tile([P, P], F32)
+            nc.vector.reciprocal(out=pen[:], in_=mask_sb[:, qt, kt * P : (kt + 1) * P])
+            nc.vector.tensor_scalar(
+                out=pen[:],
+                in0=pen[:],
+                scalar1=-1.0,
+                scalar2=-1.0 / SCALE,
+                op0=ALU.add,
+                op1=ALU.mult,
             )
-            pT_ps = psum_t.tile([P, KEY_TILES, P], F32, tag="t")
-            for kt in range(KEY_TILES):
-                nc.tensor.transpose(
-                    pT_ps[:, kt, :], penalty[:, qt, kt * P : (kt + 1) * P], ident_f32[:]
-                )
-            nc.scalar.mul(out=neg_penT[:, :, queries], in_=pT_ps[:], mul=-1.0 / SCALE)
+            penT_ps = psum_t.tile([P, P], F32, tag="t")
+            nc.tensor.transpose(penT_ps[:], pen[:], ident_f32[:])
+            nc.scalar.copy(out=neg_penT[:, kt, qt * P : (qt + 1) * P], in_=penT_ps[:])
+
+        for kt in range(KEY_TILES):
+            penalty_block(0, kt)
 
         wv_codes = const.tile([P, PASSES, XV], U32, align_bytes=64)
         wv_scales = const.tile([P, PASSES, XV], U8, align_bytes=64)
-        wv_view = Wv.rearrange("(g u p e) c -> g p u (e c)", g=PASSES, u=2, p=P, e=2)
         for g in range(PASSES):
-            wv_raw = stage.tile([P, 2, 2 * XV], BF16)
-            nc.sync.dma_start(out=wv_raw[:], in_=wv_view[g])
             wv_grouped = stage.tile([P, XV, PACK], BF16, align_bytes=64)
             nc.vector.tensor_copy(
                 out=wv_grouped[:].rearrange("p (c i) t -> p c t i", i=4),
-                in_=wv_raw[:]
+                in_=wv_raw[:, g]
                 .rearrange("p u (e c) -> p (u e) c", e=2)
                 .rearrange("p t (c i) -> p c t i", i=4),
             )
@@ -104,10 +132,7 @@ def tile_groupedqueryattention_pa_kernel(tc, xq, xk_rep, kv, mask, Wv, out):
             kv_codes = keep.tile([P, KEY_TILES, PASSES, P], U32, align_bytes=64)
             kv_scales = keep.tile([P, KEY_TILES, PASSES, P], U8, align_bytes=64)
             for t in range(KEY_TILES):
-                kv_raw = raw.tile([P, DIN], BF16)
-                first = b * SKV + t * P
-                nc.sync.dma_start(out=kv_raw[:], in_=kv_rows[first : first + P, :])
-                kv_words = kv_raw[:].bitcast(F32)
+                kv_words = kv_raw[(b, t)][:].bitcast(F32)
                 kv_grouped = stage.tile([P, PASSES * P * PACK], BF16, align_bytes=64)
                 grouped_words = kv_grouped[:].bitcast(F32).rearrange(
                     "p (g r u) -> p g r u", g=PASSES, r=P
@@ -156,22 +181,6 @@ def tile_groupedqueryattention_pa_kernel(tc, xq, xk_rep, kv, mask, Wv, out):
                 in_=v_grouped[:].rearrange("p f t -> p (f t)"),
             )
             return v_codes, v_scales
-
-        values = [project_values(b) for b in range(B)]
-
-        xk_raw = {}
-        xq_raw = {}
-        for b in range(B):
-            for kt in range(KEY_TILES):
-                xk_tile = raw.tile([P, DIMS], BF16, tag="xk", bufs=B * KEY_TILES)
-                first = b * SKV + kt * P
-                nc.sync.dma_start(out=xk_tile[:], in_=xk_rows[first : first + P, :])
-                xk_raw[(b, kt)] = xk_tile
-            for qt in range(Q_TILES):
-                xq_tile = raw.tile([P, DIMS], BF16, tag="xq", bufs=B * Q_TILES)
-                first = b * SQ + qt * P
-                nc.sync.dma_start(out=xq_tile[:], in_=xq_rows[first : first + P, :])
-                xq_raw[(b, qt)] = xq_tile
 
         qT_of, kT_of = {}, {}
         scores_of, shift_of, e_of, sum_of, eT_of = {}, {}, {}, {}, {}
@@ -278,14 +287,14 @@ def tile_groupedqueryattention_pa_kernel(tc, xq, xk_rep, kv, mask, Wv, out):
             grouped_of[n] = e_grouped
 
         def quantise(n):
-            e_codes = work.tile([P, PAIR * P], U32, align_bytes=64)
-            e_scales = work.tile([P, PAIR * P], U8, align_bytes=64)
+            e_codes = work.tile([P, PAIR * P], U32, align_bytes=64, bufs=WAITING)
+            e_scales = work.tile([P, PAIR * P], U8, align_bytes=64, bufs=WAITING)
             nc.vector.quantize_mx(
                 out=e_codes[:].bitcast(FP8X4),
                 scales=e_scales[:],
                 in_=grouped_of[n][:].rearrange("p a q t -> p (a q t)"),
             )
-            inv_sum = work.tile([P, PAIR], F32)
+            inv_sum = work.tile([P, PAIR], F32, bufs=WAITING + 1)
             nc.vector.reciprocal(out=inv_sum[:], in_=sum_of[n][:])
             codes_of[n] = (e_codes, e_scales)
             inv_sum_of[n] = inv_sum
@@ -334,14 +343,22 @@ def tile_groupedqueryattention_pa_kernel(tc, xq, xk_rep, kv, mask, Wv, out):
             if 0 <= n < N_ITEMS:
                 stage_of_item(n)
 
+        def ahead(n):
+            b, qt, pair = where(n)
+            if b == 0 and qt + 1 < Q_TILES and pair < KEY_TILES:
+                penalty_block(qt + 1, pair)
+            if b + 1 < B and qt == Q_TILES // 2 and pair == 0:
+                values[b + 1] = project_values(b + 1)
+
         prepare(0)
-        with tc.manual_schedule():
-            for k in range(N_ITEMS + LAG_OUT):
-                at(regroup, k - LAG_REGROUP)
-                at(quantise, k - LAG_QUANTISE)
-                at(finish, k - LAG_OUT)
-                at(scores, k)
-                at(exponentials, k - LAG_EXP)
-                at(transposes, k - LAG_TRANSPOSE)
-                at(multiply, k - LAG_QUANTISE)
-                at(prepare, k + 1)
+        values = {0: project_values(0)}
+        for k in range(N_ITEMS + LAG_OUT):
+            at(regroup, k - LAG_REGROUP)
+            at(quantise, k - LAG_QUANTISE)
+            at(finish, k - LAG_OUT)
+            at(scores, k)
+            at(exponentials, k - LAG_EXP)
+            at(transposes, k - LAG_TRANSPOSE)
+            at(multiply, k - LAG_QUANTISE)
+            at(prepare, k + 1)
+            at(ahead, k)

@@ -22,7 +22,6 @@ XV = 512
 REP = 4
 OWN = HEAD_DIM // REP
 GROUP = P // OWN
-N_GROUPS = HEADS // GROUP
 Q_TILES = SQ // P
 KEY_TILES = SKV // P
 PASSES = DIN // K_PASS
@@ -30,6 +29,7 @@ SCALE = HEAD_DIM ** -0.5
 
 PAIR = 2
 PAIRS = HEADS // PAIR
+HALVES = GROUP // PAIR
 N_ITEMS = B * Q_TILES * PAIRS
 LAG_EXP = 1
 LAG_TRANSPOSE = 2
@@ -81,12 +81,11 @@ def tile_groupedqueryattention_pa_kernel(tc, xq, xk_rep, kv, mask, Wv, out):
         wv_view = Wv.rearrange("(g u p e) c -> g p u (e c)", g=PASSES, u=2, p=P, e=2)
         for g in range(PASSES):
             nc.sync.dma_start(out=wv_raw[:, g], in_=wv_view[g])
-        for t in range(KEY_TILES):
-            kv_raw[(0, t)] = load_rows(kv_rows, 0, t, "kv")
+        for b in range(B):
+            for t in range(KEY_TILES):
+                kv_raw[(b, t)] = load_rows(kv_rows, b, t, "kv")
         for qt in range(1, Q_TILES):
             xq_raw[(0, qt)] = load_rows(xq_rows, 0, qt, "xq")
-        for t in range(KEY_TILES):
-            kv_raw[(1, t)] = load_rows(kv_rows, 1, t, "kv")
         for kt in range(KEY_TILES):
             xk_raw[(1, kt)] = load_rows(xk_rows, 1, kt, "xk")
         for qt in range(Q_TILES):
@@ -109,12 +108,36 @@ def tile_groupedqueryattention_pa_kernel(tc, xq, xk_rep, kv, mask, Wv, out):
             nc.tensor.transpose(penT_ps[:], pen[:], ident_f32[:])
             nc.scalar.copy(out=neg_penT[:, kt, qt * P : (qt + 1) * P], in_=penT_ps[:])
 
-        for kt in range(KEY_TILES):
-            penalty_block(0, kt)
+        qT_of, kT_of = {}, {}
+
+        def transpose_queries(b, qt):
+            qT = work.tile([P, HEADS, P], BF16, bufs=2)
+            for half in range(2):
+                heads = range(half * (HEADS // 2), (half + 1) * (HEADS // 2))
+                qT_ps = psum_t.tile([P, HEADS // 2, P], BF16, tag="t")
+                for a, h in enumerate(heads):
+                    nc.tensor.transpose(
+                        qT_ps[:, a, :], xq_raw[(b, qt)][:, h * P : (h + 1) * P], ident_bf[:]
+                    )
+                nc.scalar.copy(out=qT[:, heads[0] : heads[0] + HEADS // 2, :], in_=qT_ps[:])
+            qT_of[(b, qt)] = qT
+
+        def transpose_keys(b, pair):
+            kT = keep.tile([P, PAIR, SKV], BF16, tag="kT%d" % pair)
+            kT_ps = psum_t.tile([P, PAIR, KEY_TILES, P], BF16, tag="t")
+            for a in range(PAIR):
+                h = PAIR * pair + a
+                for kt in range(KEY_TILES):
+                    nc.tensor.transpose(
+                        kT_ps[:, a, kt, :], xk_raw[(b, kt)][:, h * P : (h + 1) * P], ident_bf[:]
+                    )
+            nc.scalar.copy(out=kT[:], in_=kT_ps[:].rearrange("p a k r -> p a (k r)"))
+            kT_of[(b, pair)] = kT
 
         wv_codes = const.tile([P, PASSES, XV], U32, align_bytes=64)
         wv_scales = const.tile([P, PASSES, XV], U8, align_bytes=64)
-        for g in range(PASSES):
+
+        def quantise_wv(g):
             wv_grouped = stage.tile([P, XV, PACK], BF16, align_bytes=64)
             nc.vector.tensor_copy(
                 out=wv_grouped[:].rearrange("p (c i) t -> p c t i", i=4),
@@ -182,9 +205,8 @@ def tile_groupedqueryattention_pa_kernel(tc, xq, xk_rep, kv, mask, Wv, out):
             )
             return v_codes, v_scales
 
-        qT_of, kT_of = {}, {}
-        scores_of, shift_of, e_of, sum_of, eT_of = {}, {}, {}, {}, {}
-        grouped_of, codes_of, inv_sum_of, o_of = {}, {}, {}, {}
+        scores_of, shift_of, e_of, eT_of, grouped_of, codes_of = {}, {}, {}, {}, {}, {}
+        sum_of, inv_sum_of, o_of = {}, {}, {}
 
         def where(n):
             b, rest = divmod(n, Q_TILES * PAIRS)
@@ -193,38 +215,14 @@ def tile_groupedqueryattention_pa_kernel(tc, xq, xk_rep, kv, mask, Wv, out):
 
         def prepare(n):
             b, qt, pair = where(n)
-            if pair == 0:
-                qT = work.tile([P, HEADS, P], BF16, bufs=2)
-                for half in range(2):
-                    qT_ps = psum_t.tile([P, HEADS // 2, P], BF16, tag="t")
-                    for a in range(HEADS // 2):
-                        h = half * (HEADS // 2) + a
-                        nc.tensor.transpose(
-                            qT_ps[:, a, :], xq_raw[(b, qt)][:, h * P : (h + 1) * P], ident_bf[:]
-                        )
-                    nc.scalar.copy(
-                        out=qT[:, half * (HEADS // 2) : (half + 1) * (HEADS // 2), :],
-                        in_=qT_ps[:],
-                    )
-                qT_of[(b, qt)] = qT
-            if qt == 0:
-                kT = keep.tile([P, PAIR, SKV], BF16, tag="kT%d" % pair)
-                kT_ps = psum_t.tile([P, PAIR, KEY_TILES, P], BF16, tag="t")
-                for a in range(PAIR):
-                    h = PAIR * pair + a
-                    for kt in range(KEY_TILES):
-                        nc.tensor.transpose(
-                            kT_ps[:, a, kt, :],
-                            xk_raw[(b, kt)][:, h * P : (h + 1) * P],
-                            ident_bf[:],
-                        )
-                nc.scalar.copy(out=kT[:], in_=kT_ps[:].rearrange("p a k r -> p a (k r)"))
-                kT_of[(b, pair)] = kT
+            if pair == 0 and (b, qt) not in qT_of:
+                transpose_queries(b, qt)
+            if (b, pair) not in kT_of:
+                transpose_keys(b, pair)
 
         def scores(n):
             b, qt, pair = where(n)
             queries = slice(qt * P, (qt + 1) * P)
-            neg_max = work.tile([P, PAIR], F32)
             banks = []
             for a in range(PAIR):
                 s_ps = psum_s.tile([P, SKV], F32, tag="s")
@@ -235,38 +233,44 @@ def tile_groupedqueryattention_pa_kernel(tc, xq, xk_rep, kv, mask, Wv, out):
                     start=True,
                     stop=False,
                 )
+                banks.append(s_ps)
+            neg_max = work.tile([P, PAIR], F32)
+            shift = work.tile([P, PAIR], F32)
+            for a in range(PAIR):
                 for kt in range(KEY_TILES):
                     nc.tensor.matmul(
-                        out=s_ps[:, kt * P : (kt + 1) * P],
+                        out=banks[a][:, kt * P : (kt + 1) * P],
                         lhsT=neg_penT[:, kt, queries],
                         rhs=ident_f32[:],
                         is_transpose=True,
                         start=False,
                         stop=(kt == KEY_TILES - 1),
                     )
+                head = slice(a, a + 1)
                 nc.vector.tensor_reduce(
-                    out=neg_max[:, a : a + 1], in_=s_ps[:], axis=AXIS.X, op=ALU.max, negate=True
+                    out=neg_max[:, head], in_=banks[a][:], axis=AXIS.X, op=ALU.max, negate=True
                 )
-                banks.append(s_ps)
-            shift = work.tile([P, PAIR], F32)
-            nc.vector.tensor_scalar_mul(out=shift[:], in0=neg_max[:], scalar1=SCALE)
+                nc.vector.tensor_scalar_mul(
+                    out=shift[:, head], in0=neg_max[:, head], scalar1=SCALE
+                )
             scores_of[n] = banks
             shift_of[n] = shift
 
         def exponentials(n):
             e_sb = work.tile([P, PAIR, SKV], BF16)
-            row_sum = work.tile([P, PAIR], F32, bufs=LAG_QUANTISE - LAG_EXP + 2)
+            if n % HALVES == 0:
+                sum_of[n // HALVES] = work.tile([P, GROUP], F32, name="row_sum", bufs=WAITING)
             for a in range(PAIR):
+                col = PAIR * (n % HALVES) + a
                 nc.scalar.activation(
                     out=e_sb[:, a, :],
                     in_=scores_of[n][a][:],
                     func=ACT.Exp,
                     bias=shift_of[n][:, a : a + 1],
                     scale=SCALE,
-                    accum_out=row_sum[:, a : a + 1],
+                    accum_out=sum_of[n // HALVES][:, col : col + 1],
                 )
             e_of[n] = e_sb
-            sum_of[n] = row_sum
 
         def transposes(n):
             eT_ps = psum_t.tile([P, PAIR, KEY_TILES, P], BF16, tag="t")
@@ -294,22 +298,21 @@ def tile_groupedqueryattention_pa_kernel(tc, xq, xk_rep, kv, mask, Wv, out):
                 scales=e_scales[:],
                 in_=grouped_of[n][:].rearrange("p a q t -> p (a q t)"),
             )
-            inv_sum = work.tile([P, PAIR], F32, bufs=WAITING + 1)
-            nc.vector.reciprocal(out=inv_sum[:], in_=sum_of[n][:])
             codes_of[n] = (e_codes, e_scales)
-            inv_sum_of[n] = inv_sum
 
         def multiply(n):
+            if n % HALVES != HALVES - 1:
+                return
             b, qt, pair = where(n)
-            e_codes, e_scales = codes_of[n]
             v_codes, v_scales = values[b]
-            hg = PAIR * pair // GROUP
+            hg = pair // HALVES
             group_cols = slice(hg * P, (hg + 1) * P)
-            o_ps = psum_o.tile([P, PAIR, GROUP * OWN], F32)
-            for a in range(PAIR):
-                queries = slice(a * P, (a + 1) * P)
+            o_ps = psum_o.tile([P, GROUP, GROUP * OWN], F32)
+            for hh in range(GROUP):
+                e_codes, e_scales = codes_of[n - (HALVES - 1) + hh // PAIR]
+                queries = slice((hh % PAIR) * P, (hh % PAIR + 1) * P)
                 nc.tensor.matmul_mx(
-                    out=o_ps[:, a, :],
+                    out=o_ps[:, hh, :],
                     lhsT=e_codes[:, queries].bitcast(FP8X4),
                     lhsT_scale=e_scales[:, queries],
                     rhs=v_codes[:, group_cols].bitcast(FP8X4),
@@ -317,26 +320,31 @@ def tile_groupedqueryattention_pa_kernel(tc, xq, xk_rep, kv, mask, Wv, out):
                     start=True,
                     stop=True,
                 )
-            o_of[n] = o_ps
+            inv_sum = work.tile([P, GROUP], F32)
+            nc.vector.reciprocal(out=inv_sum[:], in_=sum_of[n // HALVES][:])
+            o_of[n // HALVES] = o_ps
+            inv_sum_of[n // HALVES] = inv_sum
 
         def finish(n):
+            if n % HALVES != HALVES - 1:
+                return
             b, qt, pair = where(n)
-            first_own = PAIR * pair % GROUP
-            own = o_of[n][:].rearrange("p a (g c) -> p (a g) c", c=OWN)[
-                :, first_own : first_own + GROUP + 2 : GROUP + 1, :
+            hg = pair // HALVES
+            own = o_of[n // HALVES][:].rearrange("p h (g c) -> p (h g) c", c=OWN)[
+                :, 0 : GROUP * GROUP : GROUP + 1, :
             ]
-            shape = [P, PAIR, OWN, REP]
-            o_sb = work.tile(shape, F32, bufs=4)
+            shape = [P, GROUP, OWN, REP]
+            o_sb = work.tile(shape, F32)
             nc.vector.tensor_tensor(
                 out=o_sb[:],
                 in0=own.unsqueeze(3).to_broadcast(shape),
-                in1=inv_sum_of[n][:].unsqueeze(2).unsqueeze(3).to_broadcast(shape),
+                in1=inv_sum_of[n // HALVES][:].unsqueeze(2).unsqueeze(3).to_broadcast(shape),
                 op=ALU.mult,
             )
             first = b * SQ + qt * P
             nc.gpsimd.dma_start(
-                out=out_rows[first : first + P, pair * PAIR * P : (pair + 1) * PAIR * P],
-                in_=o_sb[:].rearrange("p a c r -> p (a c r)"),
+                out=out_rows[first : first + P, hg * GROUP * P : (hg + 1) * GROUP * P],
+                in_=o_sb[:].rearrange("p h c r -> p (h c r)"),
             )
 
         def at(stage_of_item, n):
@@ -350,8 +358,13 @@ def tile_groupedqueryattention_pa_kernel(tc, xq, xk_rep, kv, mask, Wv, out):
             if b + 1 < B and qt == Q_TILES // 2 and pair == 0:
                 values[b + 1] = project_values(b + 1)
 
+        for kt in range(KEY_TILES):
+            penalty_block(0, kt)
         prepare(0)
+        for g in range(PASSES):
+            quantise_wv(g)
         values = {0: project_values(0)}
+
         for k in range(N_ITEMS + LAG_OUT):
             at(regroup, k - LAG_REGROUP)
             at(quantise, k - LAG_QUANTISE)

@@ -36,7 +36,7 @@ LAG_TRANSPOSE = 2
 LAG_REGROUP = 3
 LAG_QUANTISE = 4
 LAG_OUT = 5
-VECTOR_SHARE = 3
+VECTOR_SHARE = 2
 WAITING = 6
 
 FLOPS = 2 * B * SKV * DIN * XV + 2 * 2 * B * HEADS * SQ * SKV * HEAD_DIM

@@ -36,7 +36,6 @@ LAG_TRANSPOSE = 2
 LAG_REGROUP = 3
 LAG_QUANTISE = 4
 LAG_OUT = 5
-VECTOR_SHARE = 2
 WAITING = 6
 
 FLOPS = 2 * B * SKV * DIN * XV + 2 * 2 * B * HEADS * SQ * SKV * HEAD_DIM
@@ -81,9 +80,12 @@ def tile_groupedqueryattention_pa_kernel(tc, xq, xk_rep, kv, mask, Wv, out):
         wv_view = Wv.rearrange("(g u p e) c -> g p u (e c)", g=PASSES, u=2, p=P, e=2)
         for g in range(PASSES):
             nc.sync.dma_start(out=wv_raw[:, g], in_=wv_view[g])
+        kv_view = kv_rows.rearrange("(b u p i) c -> b u i p c", b=B, u=2, i=2)
         for b in range(B):
             for t in range(KEY_TILES):
-                kv_raw[(b, t)] = load_rows(kv_rows, b, t, "kv")
+                kv_sb = raw.tile([P, DIN], BF16, tag="kv", name="kv_sb")
+                nc.sync.dma_start(out=kv_sb[:], in_=kv_view[b, t // 2, t % 2])
+                kv_raw[(b, t)] = kv_sb
         for qt in range(1, Q_TILES):
             xq_raw[(0, qt)] = load_rows(xq_rows, 0, qt, "xq")
         for kt in range(KEY_TILES):
@@ -273,21 +275,20 @@ def tile_groupedqueryattention_pa_kernel(tc, xq, xk_rep, kv, mask, Wv, out):
             e_of[n] = e_sb
 
         def transposes(n):
-            eT_ps = psum_t.tile([P, PAIR, KEY_TILES, P], BF16, tag="t")
+            eT_ps = psum_t.tile([P, PAIR, 2, P], F32, tag="t")
+            e_words = e_of[n][:].rearrange("p a k -> p (a k)").bitcast(F32)
             for a in range(PAIR):
-                for t in range(KEY_TILES):
-                    nc.tensor.transpose(
-                        eT_ps[:, a, t, :], e_of[n][:, a, t * P : (t + 1) * P], ident_bf[:]
-                    )
+                for u in range(2):
+                    w0 = (2 * a + u) * P
+                    nc.tensor.transpose(eT_ps[:, a, u, :], e_words[:, w0 : w0 + P], ident_f32[:])
             eT_of[n] = eT_ps
 
         def regroup(n):
-            e_grouped = work.tile([P, PAIR, P, PACK], BF16, align_bytes=64)
-            by_word = eT_of[n][:].rearrange("p a t q -> p a q t")
-            if n % VECTOR_SHARE == VECTOR_SHARE - 1:
-                nc.vector.tensor_copy(out=e_grouped[:], in_=by_word)
-            else:
-                nc.scalar.copy(out=e_grouped[:], in_=by_word)
+            e_grouped = work.tile([P, PAIR * P * PACK], BF16, align_bytes=64)
+            nc.scalar.copy(
+                out=e_grouped[:].bitcast(F32).rearrange("p (a q u) -> p a q u", a=PAIR, u=2),
+                in_=eT_of[n][:].rearrange("p a u q -> p a q u"),
+            )
             grouped_of[n] = e_grouped
 
         def quantise(n):
@@ -296,7 +297,7 @@ def tile_groupedqueryattention_pa_kernel(tc, xq, xk_rep, kv, mask, Wv, out):
             nc.vector.quantize_mx(
                 out=e_codes[:].bitcast(FP8X4),
                 scales=e_scales[:],
-                in_=grouped_of[n][:].rearrange("p a q t -> p (a q t)"),
+                in_=grouped_of[n][:],
             )
             codes_of[n] = (e_codes, e_scales)
 

@@ -10,7 +10,6 @@ U8 = mybir.dt.uint8
 FP8X4 = mybir.dt.float8_e4m3fn_x4
 ALU = mybir.AluOpType
 ACT = mybir.ActivationFunctionType
-AXIS = mybir.AxisListType
 
 P = 128
 PACK = 4
@@ -236,7 +235,7 @@ def tile_groupedqueryattention_pa_kernel(tc, xq, xk_rep, kv, mask, Wv, out):
                     stop=False,
                 )
                 banks.append(s_ps)
-            neg_max = work.tile([P, PAIR], F32)
+            neg_s = work.tile([P, PAIR, SKV], F32)
             shift = work.tile([P, PAIR], F32)
             for a in range(PAIR):
                 for kt in range(KEY_TILES):
@@ -248,14 +247,16 @@ def tile_groupedqueryattention_pa_kernel(tc, xq, xk_rep, kv, mask, Wv, out):
                         start=False,
                         stop=(kt == KEY_TILES - 1),
                     )
-                head = slice(a, a + 1)
-                nc.vector.tensor_reduce(
-                    out=neg_max[:, head], in_=banks[a][:], axis=AXIS.X, op=ALU.max, negate=True
+                nc.vector.tensor_scalar(
+                    out=neg_s[:, a, :],
+                    in0=banks[a][:],
+                    scalar1=-SCALE,
+                    scalar2=None,
+                    op0=ALU.mult,
+                    op1=ALU.min,
+                    accum_out=shift[:, a : a + 1],
                 )
-                nc.vector.tensor_scalar_mul(
-                    out=shift[:, head], in0=neg_max[:, head], scalar1=SCALE
-                )
-            scores_of[n] = banks
+            scores_of[n] = neg_s
             shift_of[n] = shift
 
         def exponentials(n):
@@ -266,10 +267,10 @@ def tile_groupedqueryattention_pa_kernel(tc, xq, xk_rep, kv, mask, Wv, out):
                 col = PAIR * (n % HALVES) + a
                 nc.scalar.activation(
                     out=e_sb[:, a, :],
-                    in_=scores_of[n][a][:],
+                    in_=scores_of[n][:, a, :],
                     func=ACT.Exp,
                     bias=shift_of[n][:, a : a + 1],
-                    scale=SCALE,
+                    scale=-1.0,
                     accum_out=sum_of[n // HALVES][:, col : col + 1],
                 )
             e_of[n] = e_sb
@@ -343,7 +344,7 @@ def tile_groupedqueryattention_pa_kernel(tc, xq, xk_rep, kv, mask, Wv, out):
                 op=ALU.mult,
             )
             first = b * SQ + qt * P
-            nc.gpsimd.dma_start(
+            nc.sync.dma_start(
                 out=out_rows[first : first + P, hg * GROUP * P : (hg + 1) * GROUP * P],
                 in_=o_sb[:].rearrange("p h c r -> p (h c r)"),
             )

@@ -29,13 +29,17 @@ SCALE = HEAD_DIM ** -0.5
 PAIR = 2
 PAIRS = HEADS // PAIR
 HALVES = GROUP // PAIR
-N_ITEMS = B * Q_TILES * PAIRS
-LAG_EXP = 1
-LAG_TRANSPOSE = 2
-LAG_REGROUP = 3
-LAG_QUANTISE = 4
-LAG_OUT = 5
-WAITING = 6
+ITEMS_OF_BATCH = Q_TILES * PAIRS
+N_ITEMS = B * ITEMS_OF_BATCH
+LAG_MAX = 1
+LAG_EXP = 3
+LAG_TRANSPOSE = 4
+LAG_REGROUP = 5
+LAG_QUANTISE = 6
+LAG_MULTIPLY = 10
+LAG_FINISH = 11
+WAITING = LAG_MULTIPLY - LAG_QUANTISE + 2
+SUMS = (LAG_FINISH - LAG_EXP) // HALVES + 2
 
 FLOPS = 2 * B * SKV * DIN * XV + 2 * 2 * B * HEADS * SQ * SKV * HEAD_DIM
 
@@ -44,16 +48,17 @@ def tile_groupedqueryattention_pa_kernel(tc, xq, xk_rep, kv, mask, Wv, out):
     nc = tc.nc
     xq_rows = xq.flatten_outer_dims()
     xk_rows = xk_rep.flatten_outer_dims()
-    kv_rows = kv.flatten_outer_dims()
     out_rows = out.flatten_outer_dims()
     mask_rows = mask.rearrange("a b q k -> (a b q) k")
+    kv_view = kv.flatten_outer_dims().rearrange("(b u p i) c -> b u i p c", b=B, u=2, i=2)
+    wv_view = Wv.rearrange("(g u p i) c -> g p u (i c)", g=PASSES, u=2, p=P, i=2)
 
     with ExitStack() as ctx:
         const = ctx.enter_context(tc.tile_pool(name="const", bufs=1))
-        raw = ctx.enter_context(tc.tile_pool(name="raw", bufs=B * KEY_TILES))
+        raw = ctx.enter_context(tc.tile_pool(name="raw", bufs=4))
         stage = ctx.enter_context(tc.tile_pool(name="stage", bufs=2))
         keep = ctx.enter_context(tc.tile_pool(name="keep", bufs=1))
-        work = ctx.enter_context(tc.tile_pool(name="work", bufs=3))
+        work = ctx.enter_context(tc.tile_pool(name="work", bufs=4))
         psum_s = ctx.enter_context(tc.psum_pool(name="psum_s", bufs=4))
         psum_t = ctx.enter_context(tc.psum_pool(name="psum_t", bufs=3))
         psum_o = ctx.enter_context(tc.psum_pool(name="psum_o", bufs=1))
@@ -63,40 +68,31 @@ def tile_groupedqueryattention_pa_kernel(tc, xq, xk_rep, kv, mask, Wv, out):
         ident_f32 = const.tile([P, P], F32)
         make_identity(nc, ident_f32[:])
 
-        def load_rows(rows, b, t, tag):
-            tile_sb = raw.tile([P, DIMS], BF16, tag=tag, name=tag)
-            first = (b * KEY_TILES + t) * P
-            nc.sync.dma_start(out=tile_sb[:], in_=rows[first : first + P, :])
-            return tile_sb
-
         xk_raw, xq_raw, kv_raw = {}, {}, {}
+
+        def load_keys(b, kt):
+            xk_sb = raw.tile([P, DIMS], BF16)
+            first = (b * KEY_TILES + kt) * P
+            nc.sync.dma_start(out=xk_sb[:], in_=xk_rows[first : first + P, :])
+            xk_raw[(b, kt)] = xk_sb
+
+        def load_queries(b, qt):
+            xq_sb = raw.tile([P, DIMS], BF16)
+            first = (b * Q_TILES + qt) * P
+            nc.sync.dma_start(out=xq_sb[:], in_=xq_rows[first : first + P, :])
+            xq_raw[(b, qt)] = xq_sb
+
+        def load_kv(b, t):
+            kv_sb = raw.tile([P, DIN], BF16)
+            nc.sync.dma_start(out=kv_sb[:], in_=kv_view[b, t // 2, t % 2])
+            kv_raw[(b, t)] = kv_sb
+
         mask_sb = const.tile([P, Q_TILES, SKV], BF16)
-        nc.sync.dma_start(out=mask_sb[:], in_=mask_rows.rearrange("(t p) k -> p t k", p=P))
-        for kt in range(KEY_TILES):
-            xk_raw[(0, kt)] = load_rows(xk_rows, 0, kt, "xk")
-        xq_raw[(0, 0)] = load_rows(xq_rows, 0, 0, "xq")
-        wv_raw = const.tile([P, PASSES, 2, 2 * XV], BF16)
-        wv_view = Wv.rearrange("(g u p e) c -> g p u (e c)", g=PASSES, u=2, p=P, e=2)
-        for g in range(PASSES):
-            nc.sync.dma_start(out=wv_raw[:, g], in_=wv_view[g])
-        kv_view = kv_rows.rearrange("(b u p i) c -> b u i p c", b=B, u=2, i=2)
-        for b in range(B):
-            for t in range(KEY_TILES):
-                kv_sb = raw.tile([P, DIN], BF16, tag="kv", name="kv_sb")
-                nc.sync.dma_start(out=kv_sb[:], in_=kv_view[b, t // 2, t % 2])
-                kv_raw[(b, t)] = kv_sb
-        for qt in range(1, Q_TILES):
-            xq_raw[(0, qt)] = load_rows(xq_rows, 0, qt, "xq")
-        for kt in range(KEY_TILES):
-            xk_raw[(1, kt)] = load_rows(xk_rows, 1, kt, "xk")
-        for qt in range(Q_TILES):
-            xq_raw[(1, qt)] = load_rows(xq_rows, 1, qt, "xq")
+        neg_penT = const.tile([P, Q_TILES, KEY_TILES, P], F32)
 
-        neg_penT = const.tile([P, KEY_TILES, SQ], F32)
-
-        def penalty_block(qt, kt):
-            pen = work.tile([P, P], F32)
-            nc.vector.reciprocal(out=pen[:], in_=mask_sb[:, qt, kt * P : (kt + 1) * P])
+        def penalty(qt):
+            pen = work.tile([P, SKV], F32, bufs=2)
+            nc.vector.reciprocal(out=pen[:], in_=mask_sb[:, qt, :])
             nc.vector.tensor_scalar(
                 out=pen[:],
                 in0=pen[:],
@@ -105,175 +101,217 @@ def tile_groupedqueryattention_pa_kernel(tc, xq, xk_rep, kv, mask, Wv, out):
                 op0=ALU.add,
                 op1=ALU.mult,
             )
-            penT_ps = psum_t.tile([P, P], F32, tag="t")
-            nc.tensor.transpose(penT_ps[:], pen[:], ident_f32[:])
-            nc.scalar.copy(out=neg_penT[:, kt, qt * P : (qt + 1) * P], in_=penT_ps[:])
+            penT_ps = psum_t.tile([P, KEY_TILES, P], F32, tag="t")
+            for kt in range(KEY_TILES):
+                nc.tensor.transpose(
+                    penT_ps[:, kt, :], pen[:, kt * P : (kt + 1) * P], ident_f32[:]
+                )
+            nc.scalar.copy(out=neg_penT[:, qt], in_=penT_ps[:])
 
         qT_of, kT_of = {}, {}
+        for b in range(B):
+            kT_of[b] = keep.tile([P, HEADS, SKV], BF16, name="kT%d" % b)
 
-        def transpose_queries(b, qt):
-            qT = work.tile([P, HEADS, P], BF16, bufs=2)
+        def keys_of_tile(b, kt):
             for half in range(2):
-                heads = range(half * (HEADS // 2), (half + 1) * (HEADS // 2))
-                qT_ps = psum_t.tile([P, HEADS // 2, P], BF16, tag="t")
-                for a, h in enumerate(heads):
+                heads = slice(half * (HEADS // 2), (half + 1) * (HEADS // 2))
+                kT_ps = psum_t.tile([P, HEADS // 2, P], BF16, tag="t")
+                for a in range(HEADS // 2):
+                    h = half * (HEADS // 2) + a
                     nc.tensor.transpose(
-                        qT_ps[:, a, :], xq_raw[(b, qt)][:, h * P : (h + 1) * P], ident_bf[:]
+                        kT_ps[:, a, :], xk_raw[(b, kt)][:, h * P : (h + 1) * P], ident_bf[:]
                     )
-                nc.scalar.copy(out=qT[:, heads[0] : heads[0] + HEADS // 2, :], in_=qT_ps[:])
-            qT_of[(b, qt)] = qT
+                copy = nc.scalar.copy if half == 0 else nc.vector.tensor_copy
+                copy(out=kT_of[b][:, heads, kt * P : (kt + 1) * P], in_=kT_ps[:])
 
-        def transpose_keys(b, pair):
-            kT = keep.tile([P, PAIR, SKV], BF16, tag="kT%d" % pair)
-            kT_ps = psum_t.tile([P, PAIR, KEY_TILES, P], BF16, tag="t")
-            for a in range(PAIR):
-                h = PAIR * pair + a
-                for kt in range(KEY_TILES):
-                    nc.tensor.transpose(
-                        kT_ps[:, a, kt, :], xk_raw[(b, kt)][:, h * P : (h + 1) * P], ident_bf[:]
-                    )
-            nc.scalar.copy(out=kT[:], in_=kT_ps[:].rearrange("p a k r -> p a (k r)"))
-            kT_of[(b, pair)] = kT
+        def transpose_key_head(b, h):
+            kT_ps = psum_t.tile([P, KEY_TILES, P], BF16, tag="t")
+            for kt in range(KEY_TILES):
+                nc.tensor.transpose(
+                    kT_ps[:, kt, :], xk_raw[(b, kt)][:, h * P : (h + 1) * P], ident_bf[:]
+                )
+            return kT_ps
 
+        def copy_key_head(b, h, kT_ps):
+            nc.scalar.copy(out=kT_of[b][:, h, :], in_=kT_ps[:].rearrange("p a r -> p (a r)"))
+
+        def transpose_queries(b, qt, hg):
+            if hg == 0:
+                qT_of[(b, qt)] = keep.tile([P, HEADS, P], BF16, name="qT", bufs=2)
+            qT_ps = psum_t.tile([P, GROUP, P], BF16, tag="t")
+            for a in range(GROUP):
+                h = GROUP * hg + a
+                nc.tensor.transpose(
+                    qT_ps[:, a, :], xq_raw[(b, qt)][:, h * P : (h + 1) * P], ident_bf[:]
+                )
+            return qT_ps
+
+        def copy_queries(b, qt, hg, qT_ps):
+            nc.scalar.copy(
+                out=qT_of[(b, qt)][:, GROUP * hg : GROUP * (hg + 1), :], in_=qT_ps[:]
+            )
+
+        wv_raw = const.tile([P, PASSES, 2, 2 * XV], BF16)
         wv_codes = const.tile([P, PASSES, XV], U32, align_bytes=64)
         wv_scales = const.tile([P, PASSES, XV], U8, align_bytes=64)
 
-        def quantise_wv(g):
+        def group_wv(g):
             wv_grouped = stage.tile([P, XV, PACK], BF16, align_bytes=64)
-            nc.vector.tensor_copy(
-                out=wv_grouped[:].rearrange("p (c i) t -> p c t i", i=4),
-                in_=wv_raw[:, g]
-                .rearrange("p u (e c) -> p (u e) c", e=2)
-                .rearrange("p t (c i) -> p c t i", i=4),
+            nc.gpsimd.tensor_scalar(
+                out=wv_grouped[:],
+                in0=wv_raw[:, g].rearrange("p u (i c) -> p c (u i)", i=2),
+                scalar1=1.0,
+                scalar2=0.0,
+                op0=ALU.mult,
+                op1=ALU.add,
             )
+            return wv_grouped
+
+        def quantise_wv(g, wv_grouped):
             nc.vector.quantize_mx(
                 out=wv_codes[:, g, :].bitcast(FP8X4),
                 scales=wv_scales[:, g, :],
                 in_=wv_grouped[:].rearrange("p c t -> p (c t)"),
             )
 
-        def project_values(b):
-            kv_codes = keep.tile([P, KEY_TILES, PASSES, P], U32, align_bytes=64)
-            kv_scales = keep.tile([P, KEY_TILES, PASSES, P], U8, align_bytes=64)
-            for t in range(KEY_TILES):
-                kv_words = kv_raw[(b, t)][:].bitcast(F32)
-                kv_grouped = stage.tile([P, PASSES * P * PACK], BF16, align_bytes=64)
-                grouped_words = kv_grouped[:].bitcast(F32).rearrange(
-                    "p (g r u) -> p g r u", g=PASSES, r=P
-                )
-                for half in range(PASSES // 2):
-                    kvT_ps = psum_t.tile([P, 2, 2, P], F32, tag="t")
-                    for a in range(2):
-                        for u in range(2):
-                            w0 = (2 * half + a) * (K_PASS // 2) + u * P
-                            nc.tensor.transpose(
-                                kvT_ps[:, a, u, :], kv_words[:, w0 : w0 + P], ident_f32[:]
-                            )
-                    nc.scalar.copy(
-                        out=grouped_words[:, 2 * half : 2 * half + 2, :, :],
-                        in_=kvT_ps[:].rearrange("p a u r -> p a r u"),
-                    )
-                nc.vector.quantize_mx(
-                    out=kv_codes[:, t].rearrange("p g r -> p (g r)").bitcast(FP8X4),
-                    scales=kv_scales[:, t].rearrange("p g r -> p (g r)"),
-                    in_=kv_grouped[:],
-                )
+        kv_grouped_of, kv_codes_of, v_grouped_of, values = {}, {}, {}, {}
 
-            v_grouped = stage.tile([P, XV, PACK], BF16, align_bytes=64)
-            for j in range(XV // P):
-                cols = slice(j * P, (j + 1) * P)
-                xv_ps = psum_s.tile([P, KEY_TILES, P], F32, tag="s")
-                for t in range(KEY_TILES):
-                    for g in range(PASSES):
-                        nc.tensor.matmul_mx(
-                            out=xv_ps[:, t, :],
-                            lhsT=kv_codes[:, t, g, :].bitcast(FP8X4),
-                            lhsT_scale=kv_scales[:, t, g, :],
-                            rhs=wv_codes[:, g, cols].bitcast(FP8X4),
-                            rhs_scale=wv_scales[:, g, cols],
-                            start=(g == 0),
-                            stop=(g == PASSES - 1),
-                        )
-                nc.scalar.copy(
-                    out=v_grouped[:, cols, :], in_=xv_ps[:].rearrange("p t f -> p f t")
+        def transpose_kv(b, t, half):
+            kv_words = kv_raw[(b, t)][:].bitcast(F32)
+            kvT_ps = psum_t.tile([P, 2, 2, P], F32, tag="t")
+            for a in range(2):
+                for u in range(2):
+                    w0 = (2 * half + a) * (K_PASS // 2) + u * P
+                    nc.tensor.transpose(
+                        kvT_ps[:, a, u, :], kv_words[:, w0 : w0 + P], ident_f32[:]
+                    )
+            return kvT_ps
+
+        def copy_kv(b, t, half, kvT_ps):
+            if half == 0:
+                kv_grouped_of[(b, t)] = stage.tile(
+                    [P, PASSES * P * PACK], BF16, name="kv_grouped", align_bytes=64
                 )
-            v_codes = keep.tile([P, XV], U32, align_bytes=64, tag="v_codes", bufs=B)
-            v_scales = keep.tile([P, XV], U8, align_bytes=64, tag="v_scales", bufs=B)
+            grouped_words = (
+                kv_grouped_of[(b, t)][:]
+                .bitcast(F32)
+                .rearrange("p (g r u) -> p g r u", g=PASSES, r=P)
+            )
+            nc.scalar.copy(
+                out=grouped_words[:, 2 * half : 2 * half + 2, :, :],
+                in_=kvT_ps[:].rearrange("p a u r -> p a r u"),
+            )
+
+        def quantise_kv(b, t):
+            if t == 0:
+                kv_codes = keep.tile([P, KEY_TILES, PASSES, P], U32, align_bytes=64)
+                kv_scales = keep.tile([P, KEY_TILES, PASSES, P], U8, align_bytes=64)
+                kv_codes_of[b] = (kv_codes, kv_scales)
+            kv_codes, kv_scales = kv_codes_of[b]
+            nc.vector.quantize_mx(
+                out=kv_codes[:, t].rearrange("p g r -> p (g r)").bitcast(FP8X4),
+                scales=kv_scales[:, t].rearrange("p g r -> p (g r)"),
+                in_=kv_grouped_of[(b, t)][:],
+            )
+
+        def project(b, j):
+            kv_codes, kv_scales = kv_codes_of[b]
+            cols = slice(j * P, (j + 1) * P)
+            xv_ps = psum_s.tile([P, KEY_TILES, P], F32, tag="s")
+            for t in range(KEY_TILES):
+                for g in range(PASSES):
+                    nc.tensor.matmul_mx(
+                        out=xv_ps[:, t, :],
+                        lhsT=kv_codes[:, t, g, :].bitcast(FP8X4),
+                        lhsT_scale=kv_scales[:, t, g, :],
+                        rhs=wv_codes[:, g, cols].bitcast(FP8X4),
+                        rhs_scale=wv_scales[:, g, cols],
+                        start=(g == 0),
+                        stop=(g == PASSES - 1),
+                    )
+            return xv_ps
+
+        def copy_xv(b, j, xv_ps):
+            if j == 0:
+                v_grouped_of[b] = stage.tile(
+                    [P, XV, PACK], BF16, name="v_grouped", align_bytes=64, bufs=1
+                )
+            nc.scalar.copy(
+                out=v_grouped_of[b][:, j * P : (j + 1) * P, :],
+                in_=xv_ps[:].rearrange("p t f -> p f t"),
+            )
+
+        def quantise_v(b):
+            v_codes = keep.tile([P, XV], U32, align_bytes=64, bufs=B)
+            v_scales = keep.tile([P, XV], U8, align_bytes=64, bufs=B)
             nc.vector.quantize_mx(
                 out=v_codes[:].bitcast(FP8X4),
                 scales=v_scales[:],
-                in_=v_grouped[:].rearrange("p f t -> p (f t)"),
+                in_=v_grouped_of[b][:].rearrange("p f t -> p (f t)"),
             )
-            return v_codes, v_scales
+            values[b] = (v_codes, v_scales)
 
-        scores_of, shift_of, e_of, eT_of, grouped_of, codes_of = {}, {}, {}, {}, {}, {}
+        banks_of, neg_s_of, shift_of, e_of, eT_of, grouped_of, codes_of = {}, {}, {}, {}, {}, {}, {}
         sum_of, inv_sum_of, o_of = {}, {}, {}
 
         def where(n):
-            b, rest = divmod(n, Q_TILES * PAIRS)
+            b, rest = divmod(n, ITEMS_OF_BATCH)
             qt, pair = divmod(rest, PAIRS)
             return b, qt, pair
 
-        def prepare(n):
+        def scores(n, a):
             b, qt, pair = where(n)
-            if pair == 0 and (b, qt) not in qT_of:
-                transpose_queries(b, qt)
-            if (b, pair) not in kT_of:
-                transpose_keys(b, pair)
+            h = PAIR * pair + a
+            s_ps = psum_s.tile([P, SKV], F32, tag="s")
+            nc.tensor.matmul(
+                out=s_ps[:],
+                lhsT=qT_of[(b, qt)][:, h, :],
+                rhs=kT_of[b][:, h, :],
+                start=True,
+                stop=False,
+            )
+            banks_of[(n, a)] = s_ps
 
-        def scores(n):
+        def add_penalty(n, a):
             b, qt, pair = where(n)
-            queries = slice(qt * P, (qt + 1) * P)
-            banks = []
-            for a in range(PAIR):
-                s_ps = psum_s.tile([P, SKV], F32, tag="s")
+            for kt in range(KEY_TILES):
                 nc.tensor.matmul(
-                    out=s_ps[:],
-                    lhsT=qT_of[(b, qt)][:, PAIR * pair + a, :],
-                    rhs=kT_of[(b, pair)][:, a, :],
-                    start=True,
-                    stop=False,
+                    out=banks_of[(n, a)][:, kt * P : (kt + 1) * P],
+                    lhsT=neg_penT[:, qt, kt, :],
+                    rhs=ident_f32[:],
+                    is_transpose=True,
+                    start=False,
+                    stop=(kt == KEY_TILES - 1),
                 )
-                banks.append(s_ps)
-            neg_s = work.tile([P, PAIR, SKV], F32)
-            shift = work.tile([P, PAIR], F32)
-            for a in range(PAIR):
-                for kt in range(KEY_TILES):
-                    nc.tensor.matmul(
-                        out=banks[a][:, kt * P : (kt + 1) * P],
-                        lhsT=neg_penT[:, kt, queries],
-                        rhs=ident_f32[:],
-                        is_transpose=True,
-                        start=False,
-                        stop=(kt == KEY_TILES - 1),
-                    )
-                nc.vector.tensor_scalar(
-                    out=neg_s[:, a, :],
-                    in0=banks[a][:],
-                    scalar1=-SCALE,
-                    scalar2=None,
-                    op0=ALU.mult,
-                    op1=ALU.min,
-                    accum_out=shift[:, a : a + 1],
-                )
-            scores_of[n] = neg_s
-            shift_of[n] = shift
 
-        def exponentials(n):
-            e_sb = work.tile([P, PAIR, SKV], BF16)
-            if n % HALVES == 0:
-                sum_of[n // HALVES] = work.tile([P, GROUP], F32, name="row_sum", bufs=WAITING)
-            for a in range(PAIR):
-                col = PAIR * (n % HALVES) + a
-                nc.scalar.activation(
-                    out=e_sb[:, a, :],
-                    in_=scores_of[n][:, a, :],
-                    func=ACT.Exp,
-                    bias=shift_of[n][:, a : a + 1],
-                    scale=-1.0,
-                    accum_out=sum_of[n // HALVES][:, col : col + 1],
-                )
-            e_of[n] = e_sb
+        def maximum(n, a):
+            if a == 0:
+                neg_s_of[n] = work.tile([P, PAIR, SKV], F32, name="neg_s")
+                shift_of[n] = work.tile([P, PAIR], F32, name="shift")
+            nc.vector.tensor_scalar(
+                out=neg_s_of[n][:, a, :],
+                in0=banks_of[(n, a)][:],
+                scalar1=-SCALE,
+                scalar2=None,
+                op0=ALU.mult,
+                op1=ALU.min,
+                accum_out=shift_of[n][:, a : a + 1],
+            )
+
+        def exponential(n, a):
+            if a == 0:
+                e_of[n] = work.tile([P, PAIR, SKV], BF16, name="e_sb")
+                if n % HALVES == 0:
+                    sum_of[n // HALVES] = work.tile([P, GROUP], F32, name="row_sum", bufs=SUMS)
+            col = PAIR * (n % HALVES) + a
+            nc.scalar.activation(
+                out=e_of[n][:, a, :],
+                in_=neg_s_of[n][:, a, :],
+                func=ACT.Exp,
+                bias=shift_of[n][:, a : a + 1],
+                scale=-1.0,
+                accum_out=sum_of[n // HALVES][:, col : col + 1],
+            )
 
         def transposes(n):
             eT_ps = psum_t.tile([P, PAIR, 2, P], F32, tag="t")
@@ -296,25 +334,22 @@ def tile_groupedqueryattention_pa_kernel(tc, xq, xk_rep, kv, mask, Wv, out):
             e_codes = work.tile([P, PAIR * P], U32, align_bytes=64, bufs=WAITING)
             e_scales = work.tile([P, PAIR * P], U8, align_bytes=64, bufs=WAITING)
             nc.vector.quantize_mx(
-                out=e_codes[:].bitcast(FP8X4),
-                scales=e_scales[:],
-                in_=grouped_of[n][:],
+                out=e_codes[:].bitcast(FP8X4), scales=e_scales[:], in_=grouped_of[n][:]
             )
             codes_of[n] = (e_codes, e_scales)
 
         def multiply(n):
-            if n % HALVES != HALVES - 1:
-                return
             b, qt, pair = where(n)
             v_codes, v_scales = values[b]
-            hg = pair // HALVES
+            e_codes, e_scales = codes_of[n]
+            hg, half = divmod(pair, HALVES)
             group_cols = slice(hg * P, (hg + 1) * P)
-            o_ps = psum_o.tile([P, GROUP, GROUP * OWN], F32)
-            for hh in range(GROUP):
-                e_codes, e_scales = codes_of[n - (HALVES - 1) + hh // PAIR]
-                queries = slice((hh % PAIR) * P, (hh % PAIR + 1) * P)
+            if half == 0:
+                o_of[n // HALVES] = psum_o.tile([P, GROUP, GROUP * OWN], F32, name="o_ps")
+            for a in range(PAIR):
+                queries = slice(a * P, (a + 1) * P)
                 nc.tensor.matmul_mx(
-                    out=o_ps[:, hh, :],
+                    out=o_of[n // HALVES][:, PAIR * half + a, :],
                     lhsT=e_codes[:, queries].bitcast(FP8X4),
                     lhsT_scale=e_scales[:, queries],
                     rhs=v_codes[:, group_cols].bitcast(FP8X4),
@@ -322,10 +357,10 @@ def tile_groupedqueryattention_pa_kernel(tc, xq, xk_rep, kv, mask, Wv, out):
                     start=True,
                     stop=True,
                 )
-            inv_sum = work.tile([P, GROUP], F32)
-            nc.vector.reciprocal(out=inv_sum[:], in_=sum_of[n // HALVES][:])
-            o_of[n // HALVES] = o_ps
-            inv_sum_of[n // HALVES] = inv_sum
+            if half == HALVES - 1:
+                inv_sum = work.tile([P, GROUP], F32)
+                nc.vector.reciprocal(out=inv_sum[:], in_=sum_of[n // HALVES][:])
+                inv_sum_of[n // HALVES] = inv_sum
 
         def finish(n):
             if n % HALVES != HALVES - 1:
@@ -344,36 +379,100 @@ def tile_groupedqueryattention_pa_kernel(tc, xq, xk_rep, kv, mask, Wv, out):
                 op=ALU.mult,
             )
             first = b * SQ + qt * P
-            nc.sync.dma_start(
+            nc.gpsimd.dma_start(
                 out=out_rows[first : first + P, hg * GROUP * P : (hg + 1) * GROUP * P],
                 in_=o_sb[:].rearrange("p h c r -> p (h c r)"),
             )
 
-        def at(stage_of_item, n):
-            if 0 <= n < N_ITEMS:
-                stage_of_item(n)
+        chores = {}
 
-        def ahead(n):
-            b, qt, pair = where(n)
-            if b == 0 and qt + 1 < Q_TILES and pair < KEY_TILES:
-                penalty_block(qt + 1, pair)
-            if b + 1 < B and qt == Q_TILES // 2 and pair == 0:
-                values[b + 1] = project_values(b + 1)
+        def at_step(k, chore):
+            chores.setdefault(k, []).append(chore)
 
-        for kt in range(KEY_TILES):
-            penalty_block(0, kt)
-        prepare(0)
+        def in_two_steps(k, first, second, key):
+            made = {}
+
+            def do_first():
+                made[0] = first(*key)
+
+            at_step(k + 1, lambda: second(*key, made[0]))
+            starts.setdefault(k, []).append(do_first)
+
+        starts = {}
+
+        def start_at_step(k, chore):
+            starts.setdefault(k, []).append(chore)
+
+        VALUES_0 = 2
+        VALUES_1 = 16
+        KEYS_1 = 9
         for g in range(PASSES):
-            quantise_wv(g)
-        values = {0: project_values(0)}
+            in_two_steps(VALUES_0 + g - 1, lambda g: group_wv(g), quantise_wv, (g,))
+        for t in range(KEY_TILES):
+            for half in range(2):
+                in_two_steps(VALUES_0 + t, transpose_kv, copy_kv, (0, t, half))
+                in_two_steps(VALUES_1 + 2 * t + half, transpose_kv, copy_kv, (1, t, half))
+            start_at_step(VALUES_0 + t + 1, lambda t=t: quantise_kv(0, t))
+            start_at_step(VALUES_1 + 2 * t + 3, lambda t=t: quantise_kv(1, t))
+            start_at_step(VALUES_0 + t + 2, lambda t=t: load_kv(1, t))
+        for j in range(XV // P):
+            in_two_steps(VALUES_0 + KEY_TILES + 1 + j // 2, project, copy_xv, (0, j))
+            in_two_steps(VALUES_1 + 2 * KEY_TILES + 2 + 2 * j, project, copy_xv, (1, j))
+        start_at_step(VALUES_0 + KEY_TILES + 3, lambda: quantise_v(0))
+        start_at_step(VALUES_1 + 2 * KEY_TILES + 10, lambda: quantise_v(1))
+        for h in range(HEADS):
+            in_two_steps(KEYS_1 + 3 * h // 2, transpose_key_head, copy_key_head, (1, h))
+        for tile in range(1, B * Q_TILES):
+            for hg in range(HEADS // GROUP):
+                in_two_steps(
+                    PAIRS * (tile - 1) + 3 + hg,
+                    transpose_queries,
+                    copy_queries,
+                    (tile // Q_TILES, tile % Q_TILES, hg),
+                )
+        for qt in range(Q_TILES):
+            start_at_step(PAIRS * qt, lambda qt=qt: load_queries(1, qt))
 
-        for k in range(N_ITEMS + LAG_OUT):
-            at(regroup, k - LAG_REGROUP)
-            at(quantise, k - LAG_QUANTISE)
-            at(finish, k - LAG_OUT)
-            at(scores, k)
-            at(exponentials, k - LAG_EXP)
-            at(transposes, k - LAG_TRANSPOSE)
-            at(multiply, k - LAG_QUANTISE)
-            at(prepare, k + 1)
-            at(ahead, k)
+        nc.sync.dma_start(out=mask_sb[:], in_=mask_rows.rearrange("(t p) k -> p t k", p=P))
+        for kt in range(KEY_TILES):
+            load_keys(0, kt)
+        load_queries(0, 0)
+        for g in range(PASSES):
+            nc.sync.dma_start(out=wv_raw[:, g], in_=wv_view[g])
+        for t in range(KEY_TILES):
+            load_kv(0, t)
+        for qt in range(1, Q_TILES):
+            load_queries(0, qt)
+
+        with tc.manual_schedule():
+            for qt in range(Q_TILES):
+                penalty(qt)
+            for kt in range(KEY_TILES):
+                keys_of_tile(0, kt)
+            for hg in range(HEADS // GROUP):
+                copy_queries(0, 0, hg, transpose_queries(0, 0, hg))
+            for kt in range(KEY_TILES):
+                load_keys(1, kt)
+
+            def at(stage_of_item, n, *rest):
+                if 0 <= n < N_ITEMS:
+                    stage_of_item(n, *rest)
+
+            for k in range(N_ITEMS + LAG_FINISH):
+                at(finish, k - LAG_FINISH)
+                at(regroup, k - LAG_REGROUP)
+                at(maximum, k - LAG_MAX, 0)
+                at(transposes, k - LAG_TRANSPOSE)
+                at(quantise, k - LAG_QUANTISE)
+                at(maximum, k - LAG_MAX, 1)
+                at(scores, k, 0)
+                at(multiply, k - LAG_MULTIPLY)
+                at(scores, k, 1)
+                at(add_penalty, k, 0)
+                at(add_penalty, k, 1)
+                at(exponential, k - LAG_EXP, 0)
+                at(exponential, k - LAG_EXP, 1)
+                for chore in chores.get(k, []):
+                    chore()
+                for chore in starts.get(k, []):
+                    chore()

@@ -90,8 +90,11 @@ def tile_groupedqueryattention_pa_kernel(tc, xq, xk_rep, kv, mask, Wv, out):
         mask_sb = const.tile([P, Q_TILES, SKV], BF16)
         neg_penT = const.tile([P, Q_TILES, KEY_TILES, P], F32)
 
+        pen_of = {}
+
         def penalty(qt):
             pen = work.tile([P, SKV], F32, bufs=2)
+            pen_of[qt] = pen
             nc.vector.reciprocal(out=pen[:], in_=mask_sb[:, qt, :])
             nc.vector.tensor_scalar(
                 out=pen[:],
@@ -101,11 +104,16 @@ def tile_groupedqueryattention_pa_kernel(tc, xq, xk_rep, kv, mask, Wv, out):
                 op0=ALU.add,
                 op1=ALU.mult,
             )
+
+        def transpose_penalty(qt):
             penT_ps = psum_t.tile([P, KEY_TILES, P], F32, tag="t")
             for kt in range(KEY_TILES):
                 nc.tensor.transpose(
-                    penT_ps[:, kt, :], pen[:, kt * P : (kt + 1) * P], ident_f32[:]
+                    penT_ps[:, kt, :], pen_of[qt][:, kt * P : (kt + 1) * P], ident_f32[:]
                 )
+            return penT_ps
+
+        def copy_penalty(qt, penT_ps):
             nc.scalar.copy(out=neg_penT[:, qt], in_=penT_ps[:])
 
         qT_of, kT_of = {}, {}
@@ -127,8 +135,12 @@ def tile_groupedqueryattention_pa_kernel(tc, xq, xk_rep, kv, mask, Wv, out):
         def transpose_key_head(b, h):
             kT_ps = psum_t.tile([P, KEY_TILES, P], BF16, tag="t")
             for kt in range(KEY_TILES):
-                nc.tensor.transpose(
-                    kT_ps[:, kt, :], xk_raw[(b, kt)][:, h * P : (h + 1) * P], ident_bf[:]
+                nc.tensor.matmul(
+                    out=kT_ps[:, kt, :],
+                    lhsT=xk_raw[(b, kt)][:, h * P : (h + 1) * P],
+                    rhs=ident_bf[:],
+                    start=True,
+                    stop=True,
                 )
             return kT_ps
 
@@ -384,28 +396,29 @@ def tile_groupedqueryattention_pa_kernel(tc, xq, xk_rep, kv, mask, Wv, out):
                 in_=o_sb[:].rearrange("p h c r -> p (h c r)"),
             )
 
-        chores = {}
+        with_scores, chores, starts = {}, {}, {}
 
         def at_step(k, chore):
             chores.setdefault(k, []).append(chore)
 
-        def in_two_steps(k, first, second, key):
+        def start_at_step(k, chore):
+            starts.setdefault(k, []).append(chore)
+
+        def in_two_steps(k, first, second, key, place=starts):
             made = {}
 
             def do_first():
                 made[0] = first(*key)
 
+            place.setdefault(k, []).append(do_first)
             at_step(k + 1, lambda: second(*key, made[0]))
-            starts.setdefault(k, []).append(do_first)
-
-        starts = {}
-
-        def start_at_step(k, chore):
-            starts.setdefault(k, []).append(chore)
 
         VALUES_0 = 2
         VALUES_1 = 16
-        KEYS_1 = 9
+        KEYS_1 = 7
+        for qt in range(1, Q_TILES):
+            start_at_step(PAIRS * qt - 6, lambda qt=qt: penalty(qt))
+            in_two_steps(PAIRS * qt - 5, transpose_penalty, copy_penalty, (qt,))
         for g in range(PASSES):
             in_two_steps(VALUES_0 + g - 1, lambda g: group_wv(g), quantise_wv, (g,))
         for t in range(KEY_TILES):
@@ -421,11 +434,11 @@ def tile_groupedqueryattention_pa_kernel(tc, xq, xk_rep, kv, mask, Wv, out):
         start_at_step(VALUES_0 + KEY_TILES + 3, lambda: quantise_v(0))
         start_at_step(VALUES_1 + 2 * KEY_TILES + 10, lambda: quantise_v(1))
         for h in range(HEADS):
-            in_two_steps(KEYS_1 + 3 * h // 2, transpose_key_head, copy_key_head, (1, h))
+            in_two_steps(KEYS_1 + 2 * h, transpose_key_head, copy_key_head, (1, h), with_scores)
         for tile in range(1, B * Q_TILES):
             for hg in range(HEADS // GROUP):
                 in_two_steps(
-                    PAIRS * (tile - 1) + 3 + hg,
+                    PAIRS * (tile - 1) + 2 * hg,
                     transpose_queries,
                     copy_queries,
                     (tile // Q_TILES, tile % Q_TILES, hg),
@@ -433,20 +446,23 @@ def tile_groupedqueryattention_pa_kernel(tc, xq, xk_rep, kv, mask, Wv, out):
         for qt in range(Q_TILES):
             start_at_step(PAIRS * qt, lambda qt=qt: load_queries(1, qt))
 
-        nc.sync.dma_start(out=mask_sb[:], in_=mask_rows.rearrange("(t p) k -> p t k", p=P))
+        mask_view = mask_rows.rearrange("(t p) k -> p t k", p=P)
+        nc.sync.dma_start(out=mask_sb[:, 0], in_=mask_view[:, 0])
         for kt in range(KEY_TILES):
             load_keys(0, kt)
         load_queries(0, 0)
+        nc.sync.dma_start(out=mask_sb[:, 1:], in_=mask_view[:, 1:])
+        load_queries(0, 1)
         for g in range(PASSES):
             nc.sync.dma_start(out=wv_raw[:, g], in_=wv_view[g])
         for t in range(KEY_TILES):
             load_kv(0, t)
-        for qt in range(1, Q_TILES):
+        for qt in range(2, Q_TILES):
             load_queries(0, qt)
 
         with tc.manual_schedule():
-            for qt in range(Q_TILES):
-                penalty(qt)
+            penalty(0)
+            copy_penalty(0, transpose_penalty(0))
             for kt in range(KEY_TILES):
                 keys_of_tile(0, kt)
             for hg in range(HEADS // GROUP):
@@ -465,6 +481,8 @@ def tile_groupedqueryattention_pa_kernel(tc, xq, xk_rep, kv, mask, Wv, out):
                 at(transposes, k - LAG_TRANSPOSE)
                 at(quantise, k - LAG_QUANTISE)
                 at(maximum, k - LAG_MAX, 1)
+                for chore in with_scores.get(k, []):
+                    chore()
                 at(scores, k, 0)
                 at(multiply, k - LAG_MULTIPLY)
                 at(scores, k, 1)

@@ -27,19 +27,28 @@ PASSES = DIN // K_PASS
 SCALE = HEAD_DIM ** -0.5
 
 PAIR = 2
-PAIRS = HEADS // PAIR
 HALVES = GROUP // PAIR
-ITEMS_OF_BATCH = Q_TILES * PAIRS
-N_ITEMS = B * ITEMS_OF_BATCH
+GROUPS = B * HEADS // GROUP
+ITEMS_OF_GROUP = Q_TILES * HALVES
+N_ITEMS = GROUPS * ITEMS_OF_GROUP
 LAG_MAX = 1
 LAG_EXP = 3
 LAG_TRANSPOSE = 4
 LAG_REGROUP = 5
 LAG_QUANTISE = 6
-LAG_MULTIPLY = 10
-LAG_FINISH = 11
+LAG_MULTIPLY = 17
+LAG_MULTIPLY_LAST = 9
+
+
+def multiply_step(n):
+    if n < N_ITEMS // 2:
+        return n + LAG_MULTIPLY
+    first = N_ITEMS // 2 + LAG_MULTIPLY
+    return max(first + (n - N_ITEMS // 2) // 2, n + LAG_MULTIPLY_LAST)
+
+
 WAITING = LAG_MULTIPLY - LAG_QUANTISE + 2
-SUMS = (LAG_FINISH - LAG_EXP) // HALVES + 2
+SUMS = (LAG_MULTIPLY - LAG_EXP) // HALVES + 2
 
 FLOPS = 2 * B * SKV * DIN * XV + 2 * 2 * B * HEADS * SQ * SKV * HEAD_DIM
 
@@ -70,17 +79,18 @@ def tile_groupedqueryattention_pa_kernel(tc, xq, xk_rep, kv, mask, Wv, out):
 
         xk_raw, xq_raw, kv_raw = {}, {}, {}
 
-        def load_keys(b, kt):
-            xk_sb = raw.tile([P, DIMS], BF16)
-            first = (b * KEY_TILES + kt) * P
-            nc.sync.dma_start(out=xk_sb[:], in_=xk_rows[first : first + P, :])
-            xk_raw[(b, kt)] = xk_sb
+        def rows_of_group(rows, g):
+            b, hg = divmod(g, HEADS // GROUP)
+            cols = slice(hg * GROUP * P, (hg + 1) * GROUP * P)
+            return rows[b * SQ : (b + 1) * SQ, cols].rearrange("(t p) c -> p t c", p=P)
 
-        def load_queries(b, qt):
-            xq_sb = raw.tile([P, DIMS], BF16)
-            first = (b * Q_TILES + qt) * P
-            nc.sync.dma_start(out=xq_sb[:], in_=xq_rows[first : first + P, :])
-            xq_raw[(b, qt)] = xq_sb
+        def load_group(g):
+            xk_sb = raw.tile([P, KEY_TILES, GROUP * P], BF16, bufs=3)
+            nc.sync.dma_start(out=xk_sb[:], in_=rows_of_group(xk_rows, g))
+            xk_raw[g] = xk_sb
+            xq_sb = raw.tile([P, Q_TILES, GROUP * P], BF16, bufs=3)
+            nc.sync.dma_start(out=xq_sb[:], in_=rows_of_group(xq_rows, g))
+            xq_raw[g] = xq_sb
 
         def load_kv(b, t):
             kv_sb = raw.tile([P, DIN], BF16)
@@ -117,51 +127,69 @@ def tile_groupedqueryattention_pa_kernel(tc, xq, xk_rep, kv, mask, Wv, out):
             nc.scalar.copy(out=neg_penT[:, qt], in_=penT_ps[:])
 
         qT_of, kT_of = {}, {}
-        for b in range(B):
-            kT_of[b] = keep.tile([P, HEADS, SKV], BF16, name="kT%d" % b)
 
-        def keys_of_tile(b, kt):
-            for half in range(2):
-                heads = slice(half * (HEADS // 2), (half + 1) * (HEADS // 2))
-                kT_ps = psum_t.tile([P, HEADS // 2, P], BF16, tag="t")
-                for a in range(HEADS // 2):
-                    h = half * (HEADS // 2) + a
-                    nc.tensor.transpose(
-                        kT_ps[:, a, :], xk_raw[(b, kt)][:, h * P : (h + 1) * P], ident_bf[:]
-                    )
-                copy = nc.scalar.copy if half == 0 else nc.vector.tensor_copy
-                copy(out=kT_of[b][:, heads, kt * P : (kt + 1) * P], in_=kT_ps[:])
+        def new_group(g):
+            kT_of[g] = work.tile([P, GROUP, SKV], BF16, name="kT", bufs=2)
+            qT_of[g] = work.tile([P, Q_TILES, GROUP, P], BF16, name="qT", bufs=2)
 
-        def transpose_key_head(b, h):
+        def transpose_key_head(g, a):
             kT_ps = psum_t.tile([P, KEY_TILES, P], BF16, tag="t")
             for kt in range(KEY_TILES):
+                nc.tensor.transpose(
+                    kT_ps[:, kt, :], xk_raw[g][:, kt, a * P : (a + 1) * P], ident_bf[:]
+                )
+            return kT_ps
+
+        def copy_key_head(g, a, kT_ps):
+            nc.vector.tensor_copy(
+                out=kT_of[g][:, a, :], in_=kT_ps[:].rearrange("p t r -> p (t r)")
+            )
+
+        PARK = SKV // 2
+
+        def parked(g):
+            return out_rows[B * SQ - P : B * SQ, g * PARK : (g + 1) * PARK]
+
+        def transpose_keys(g):
+            kc_ps = psum_t.tile([P, KEY_TILES, P], BF16, tag="t")
+            for kt in range(KEY_TILES):
+                different = xk_raw[g][:, kt, :].rearrange("p (c r) -> p c r", r=REP)[:, :, 0]
+                nc.tensor.transpose(kc_ps[:, kt, :], different, ident_bf[:])
+            return kc_ps
+
+        def spread_keys(g, kc_ps):
+            new_group(g)
+            kc_sb = work.tile([P, SKV], BF16, bufs=2)
+            nc.scalar.copy(out=kc_sb[:], in_=kc_ps[:].rearrange("p t r -> p (t r)"))
+            nc.sync.dma_start(out=parked(g), in_=kc_sb[:].bitcast(F32))
+            kT_words = kT_of[g][:].bitcast(F32)
+            for r in range(REP):
+                nc.sync.dma_start(
+                    out=kT_words[r:P:REP, :, :], in_=parked(g).rearrange("(a j) w -> j a w", a=GROUP)
+                )
+
+        def transpose_queries(g, qt):
+            qT_ps = psum_t.tile([P, GROUP, P], BF16, tag="t")
+            for a in range(GROUP):
+                nc.tensor.transpose(
+                    qT_ps[:, a, :], xq_raw[g][:, qt, a * P : (a + 1) * P], ident_bf[:]
+                )
+            return qT_ps
+
+        def multiply_queries(g, qt):
+            qT_ps = psum_t.tile([P, GROUP, P], BF16, tag="t")
+            for a in range(GROUP):
                 nc.tensor.matmul(
-                    out=kT_ps[:, kt, :],
-                    lhsT=xk_raw[(b, kt)][:, h * P : (h + 1) * P],
+                    out=qT_ps[:, a, :],
+                    lhsT=xq_raw[g][:, qt, a * P : (a + 1) * P],
                     rhs=ident_bf[:],
                     start=True,
                     stop=True,
                 )
-            return kT_ps
-
-        def copy_key_head(b, h, kT_ps):
-            nc.scalar.copy(out=kT_of[b][:, h, :], in_=kT_ps[:].rearrange("p a r -> p (a r)"))
-
-        def transpose_queries(b, qt, hg):
-            if hg == 0:
-                qT_of[(b, qt)] = keep.tile([P, HEADS, P], BF16, name="qT", bufs=2)
-            qT_ps = psum_t.tile([P, GROUP, P], BF16, tag="t")
-            for a in range(GROUP):
-                h = GROUP * hg + a
-                nc.tensor.transpose(
-                    qT_ps[:, a, :], xq_raw[(b, qt)][:, h * P : (h + 1) * P], ident_bf[:]
-                )
             return qT_ps
 
-        def copy_queries(b, qt, hg, qT_ps):
-            nc.scalar.copy(
-                out=qT_of[(b, qt)][:, GROUP * hg : GROUP * (hg + 1), :], in_=qT_ps[:]
-            )
+        def copy_queries(g, qt, qT_ps):
+            nc.scalar.copy(out=qT_of[g][:, qt], in_=qT_ps[:])
 
         wv_raw = const.tile([P, PASSES, 2, 2 * XV], BF16)
         wv_codes = const.tile([P, PASSES, XV], U32, align_bytes=64)
@@ -267,25 +295,25 @@ def tile_groupedqueryattention_pa_kernel(tc, xq, xk_rep, kv, mask, Wv, out):
         sum_of, inv_sum_of, o_of = {}, {}, {}
 
         def where(n):
-            b, rest = divmod(n, ITEMS_OF_BATCH)
-            qt, pair = divmod(rest, PAIRS)
-            return b, qt, pair
+            g, rest = divmod(n, ITEMS_OF_GROUP)
+            qt, half = divmod(rest, HALVES)
+            return g, qt, half
 
         def scores(n, a):
-            b, qt, pair = where(n)
-            h = PAIR * pair + a
+            g, qt, half = where(n)
+            head = PAIR * half + a
             s_ps = psum_s.tile([P, SKV], F32, tag="s")
             nc.tensor.matmul(
                 out=s_ps[:],
-                lhsT=qT_of[(b, qt)][:, h, :],
-                rhs=kT_of[b][:, h, :],
+                lhsT=qT_of[g][:, qt, head, :],
+                rhs=kT_of[g][:, head, :],
                 start=True,
                 stop=False,
             )
             banks_of[(n, a)] = s_ps
 
         def add_penalty(n, a):
-            b, qt, pair = where(n)
+            g, qt, half = where(n)
             for kt in range(KEY_TILES):
                 nc.tensor.matmul(
                     out=banks_of[(n, a)][:, kt * P : (kt + 1) * P],
@@ -351,10 +379,10 @@ def tile_groupedqueryattention_pa_kernel(tc, xq, xk_rep, kv, mask, Wv, out):
             codes_of[n] = (e_codes, e_scales)
 
         def multiply(n):
-            b, qt, pair = where(n)
+            g, qt, half = where(n)
+            b, hg = divmod(g, HEADS // GROUP)
             v_codes, v_scales = values[b]
             e_codes, e_scales = codes_of[n]
-            hg, half = divmod(pair, HALVES)
             group_cols = slice(hg * P, (hg + 1) * P)
             if half == 0:
                 o_of[n // HALVES] = psum_o.tile([P, GROUP, GROUP * OWN], F32, name="o_ps")
@@ -377,8 +405,8 @@ def tile_groupedqueryattention_pa_kernel(tc, xq, xk_rep, kv, mask, Wv, out):
         def finish(n):
             if n % HALVES != HALVES - 1:
                 return
-            b, qt, pair = where(n)
-            hg = pair // HALVES
+            g, qt, half = where(n)
+            b, hg = divmod(g, HEADS // GROUP)
             own = o_of[n // HALVES][:].rearrange("p h (g c) -> p (h g) c", c=OWN)[
                 :, 0 : GROUP * GROUP : GROUP + 1, :
             ]
@@ -396,86 +424,92 @@ def tile_groupedqueryattention_pa_kernel(tc, xq, xk_rep, kv, mask, Wv, out):
                 in_=o_sb[:].rearrange("p h c r -> p (h c r)"),
             )
 
-        with_scores, chores, starts = {}, {}, {}
+        with_scores, copies, starts, late_copies = {}, {}, {}, {}
 
-        def at_step(k, chore):
-            chores.setdefault(k, []).append(chore)
+        def at_step(place, k, chore):
+            place.setdefault(k, []).append(chore)
 
-        def start_at_step(k, chore):
-            starts.setdefault(k, []).append(chore)
-
-        def in_two_steps(k, first, second, key, place=starts):
+        def in_two_steps(k, first, second, key):
             made = {}
+            at_step(starts, k, lambda: made.update(x=first(*key)))
+            at_step(copies, k + 1, lambda: second(*key, made["x"]))
 
-            def do_first():
-                made[0] = first(*key)
+        def in_one_step(k, first, second, key):
+            made = {}
+            at_step(with_scores, k, lambda: made.update(x=first(*key)))
+            at_step(late_copies, k, lambda: second(*key, made["x"]))
 
-            place.setdefault(k, []).append(do_first)
-            at_step(k + 1, lambda: second(*key, made[0]))
+        BY_MATMUL = N_ITEMS // 2
 
-        VALUES_0 = 2
-        VALUES_1 = 16
-        KEYS_1 = 7
+        def prepare_queries(k, g, qt):
+            if k < BY_MATMUL:
+                in_one_step(k, multiply_queries, copy_queries, (g, qt))
+            else:
+                in_two_steps(k, transpose_queries, copy_queries, (g, qt))
+
         for qt in range(1, Q_TILES):
-            start_at_step(PAIRS * qt - 6, lambda qt=qt: penalty(qt))
-            in_two_steps(PAIRS * qt - 5, transpose_penalty, copy_penalty, (qt,))
+            at_step(starts, HALVES * (qt - 1), lambda qt=qt: penalty(qt))
+            in_two_steps(HALVES * (qt - 1), transpose_penalty, copy_penalty, (qt,))
+            prepare_queries(qt - 1, 0, qt)
+        for g in range(1, GROUPS):
+            before = ITEMS_OF_GROUP * (g - 1)
+            in_two_steps(before, transpose_keys, spread_keys, (g,))
+            for qt in range(Q_TILES):
+                prepare_queries(before + 2 * qt + 1, g, qt)
+            if g + 1 < GROUPS and g > 1:
+                at_step(starts, before, lambda g=g: load_group(g + 1))
+        VALUES_0 = 3
+        VALUES_1 = 17
+        for c in range(2 * KEY_TILES):
+            t, half = divmod(c, 2)
+            in_two_steps(VALUES_0 + c, transpose_kv, copy_kv, (0, t, half))
+            in_two_steps(VALUES_1 + 2 * c, transpose_kv, copy_kv, (1, t, half))
+            if half == 1:
+                at_step(starts, VALUES_0 + c + 1, lambda t=t: quantise_kv(0, t))
+                at_step(starts, VALUES_0 + c + 1, lambda t=t: load_kv(1, t))
+                at_step(starts, VALUES_1 + 2 * c + 1, lambda t=t: quantise_kv(1, t))
         for g in range(PASSES):
-            in_two_steps(VALUES_0 + g - 1, lambda g: group_wv(g), quantise_wv, (g,))
-        for t in range(KEY_TILES):
-            for half in range(2):
-                in_two_steps(VALUES_0 + t, transpose_kv, copy_kv, (0, t, half))
-                in_two_steps(VALUES_1 + 2 * t + half, transpose_kv, copy_kv, (1, t, half))
-            start_at_step(VALUES_0 + t + 1, lambda t=t: quantise_kv(0, t))
-            start_at_step(VALUES_1 + 2 * t + 3, lambda t=t: quantise_kv(1, t))
-            start_at_step(VALUES_0 + t + 2, lambda t=t: load_kv(1, t))
+            in_two_steps(1 + g, group_wv, quantise_wv, (g,))
+        PROJECT_0 = VALUES_0 + 2 * KEY_TILES + 1
+        PROJECT_1 = VALUES_1 + 4 * KEY_TILES + 1
         for j in range(XV // P):
-            in_two_steps(VALUES_0 + KEY_TILES + 1 + j // 2, project, copy_xv, (0, j))
-            in_two_steps(VALUES_1 + 2 * KEY_TILES + 2 + 2 * j, project, copy_xv, (1, j))
-        start_at_step(VALUES_0 + KEY_TILES + 3, lambda: quantise_v(0))
-        start_at_step(VALUES_1 + 2 * KEY_TILES + 10, lambda: quantise_v(1))
-        for h in range(HEADS):
-            in_two_steps(KEYS_1 + 2 * h, transpose_key_head, copy_key_head, (1, h), with_scores)
-        for tile in range(1, B * Q_TILES):
-            for hg in range(HEADS // GROUP):
-                in_two_steps(
-                    PAIRS * (tile - 1) + 2 * hg,
-                    transpose_queries,
-                    copy_queries,
-                    (tile // Q_TILES, tile % Q_TILES, hg),
-                )
-        for qt in range(Q_TILES):
-            start_at_step(PAIRS * qt, lambda qt=qt: load_queries(1, qt))
+            made_0, made_1 = {}, {}
+            for b, k, made in ((0, PROJECT_0 + j, made_0), (1, PROJECT_1 + 2 * j, made_1)):
+                at_step(with_scores, k, lambda b=b, j=j, made=made: made.update(x=project(b, j)))
+                at_step(copies, k + 1, lambda b=b, j=j, made=made: copy_xv(b, j, made["x"]))
+        at_step(starts, PROJECT_0 + XV // P, lambda: quantise_v(0))
+        at_step(starts, PROJECT_1 + 2 * (XV // P) - 1, lambda: quantise_v(1))
 
         mask_view = mask_rows.rearrange("(t p) k -> p t k", p=P)
         nc.sync.dma_start(out=mask_sb[:, 0], in_=mask_view[:, 0])
-        for kt in range(KEY_TILES):
-            load_keys(0, kt)
-        load_queries(0, 0)
+        load_group(0)
         nc.sync.dma_start(out=mask_sb[:, 1:], in_=mask_view[:, 1:])
-        load_queries(0, 1)
+        load_group(1)
         for g in range(PASSES):
             nc.sync.dma_start(out=wv_raw[:, g], in_=wv_view[g])
         for t in range(KEY_TILES):
             load_kv(0, t)
-        for qt in range(2, Q_TILES):
-            load_queries(0, qt)
+        load_group(2)
 
         with tc.manual_schedule():
             penalty(0)
+            new_group(0)
+            for a in range(GROUP):
+                copy_key_head(0, a, transpose_key_head(0, a))
+                if a == 0:
+                    copy_queries(0, 0, transpose_queries(0, 0))
             copy_penalty(0, transpose_penalty(0))
-            for kt in range(KEY_TILES):
-                keys_of_tile(0, kt)
-            for hg in range(HEADS // GROUP):
-                copy_queries(0, 0, hg, transpose_queries(0, 0, hg))
-            for kt in range(KEY_TILES):
-                load_keys(1, kt)
 
             def at(stage_of_item, n, *rest):
                 if 0 <= n < N_ITEMS:
                     stage_of_item(n, *rest)
 
-            for k in range(N_ITEMS + LAG_FINISH):
-                at(finish, k - LAG_FINISH)
+            multiplies = {}
+            for n in range(N_ITEMS):
+                multiplies.setdefault(multiply_step(n), []).append(n)
+            for k in range(multiply_step(N_ITEMS - 1) + 2):
+                for n in multiplies.get(k - 1, []):
+                    finish(n)
                 at(regroup, k - LAG_REGROUP)
                 at(maximum, k - LAG_MAX, 0)
                 at(transposes, k - LAG_TRANSPOSE)
@@ -484,13 +518,13 @@ def tile_groupedqueryattention_pa_kernel(tc, xq, xk_rep, kv, mask, Wv, out):
                 for chore in with_scores.get(k, []):
                     chore()
                 at(scores, k, 0)
-                at(multiply, k - LAG_MULTIPLY)
+                for n in multiplies.get(k, []):
+                    multiply(n)
                 at(scores, k, 1)
                 at(add_penalty, k, 0)
                 at(add_penalty, k, 1)
                 at(exponential, k - LAG_EXP, 0)
                 at(exponential, k - LAG_EXP, 1)
-                for chore in chores.get(k, []):
-                    chore()
-                for chore in starts.get(k, []):
-                    chore()
+                for place in (copies, starts, late_copies):
+                    for chore in place.get(k, []):
+                        chore()

@@ -37,7 +37,7 @@ LAG_TRANSPOSE = 4
 LAG_REGROUP = 5
 LAG_QUANTISE = 6
 LAG_MULTIPLY = 17
-LAG_MULTIPLY_LAST = 9
+LAG_MULTIPLY_LAST = LAG_QUANTISE + 1
 
 
 def multiply_step(n):
@@ -47,6 +47,7 @@ def multiply_step(n):
     return max(first + (n - N_ITEMS // 2) // 2, n + LAG_MULTIPLY_LAST)
 
 
+WARM_UP = 10
 WAITING = LAG_MULTIPLY - LAG_QUANTISE + 2
 SUMS = (LAG_MULTIPLY - LAG_EXP) // HALVES + 2
 
@@ -84,12 +85,14 @@ def tile_groupedqueryattention_pa_kernel(tc, xq, xk_rep, kv, mask, Wv, out):
             cols = slice(hg * GROUP * P, (hg + 1) * GROUP * P)
             return rows[b * SQ : (b + 1) * SQ, cols].rearrange("(t p) c -> p t c", p=P)
 
-        def load_group(g):
+        def load_group(g, pieces=((0, Q_TILES),)):
             xk_sb = raw.tile([P, KEY_TILES, GROUP * P], BF16, bufs=3)
-            nc.sync.dma_start(out=xk_sb[:], in_=rows_of_group(xk_rows, g))
-            xk_raw[g] = xk_sb
             xq_sb = raw.tile([P, Q_TILES, GROUP * P], BF16, bufs=3)
-            nc.sync.dma_start(out=xq_sb[:], in_=rows_of_group(xq_rows, g))
+            for tile_sb, rows in ((xk_sb, xk_rows), (xq_sb, xq_rows)):
+                view = rows_of_group(rows, g)
+                for lo, hi in pieces:
+                    nc.sync.dma_start(out=tile_sb[:, lo:hi], in_=view[:, lo:hi])
+            xk_raw[g] = xk_sb
             xq_raw[g] = xq_sb
 
         def load_kv(b, t):
@@ -132,18 +135,16 @@ def tile_groupedqueryattention_pa_kernel(tc, xq, xk_rep, kv, mask, Wv, out):
             kT_of[g] = work.tile([P, GROUP, SKV], BF16, name="kT", bufs=2)
             qT_of[g] = work.tile([P, Q_TILES, GROUP, P], BF16, name="qT", bufs=2)
 
-        def transpose_key_head(g, a):
-            kT_ps = psum_t.tile([P, KEY_TILES, P], BF16, tag="t")
-            for kt in range(KEY_TILES):
+        def transpose_key_tile(g, kt):
+            kT_ps = psum_t.tile([P, GROUP, P], BF16, tag="t")
+            for a in range(GROUP):
                 nc.tensor.transpose(
-                    kT_ps[:, kt, :], xk_raw[g][:, kt, a * P : (a + 1) * P], ident_bf[:]
+                    kT_ps[:, a, :], xk_raw[g][:, kt, a * P : (a + 1) * P], ident_bf[:]
                 )
             return kT_ps
 
-        def copy_key_head(g, a, kT_ps):
-            nc.vector.tensor_copy(
-                out=kT_of[g][:, a, :], in_=kT_ps[:].rearrange("p t r -> p (t r)")
-            )
+        def copy_key_tile(g, kt, kT_ps):
+            nc.vector.tensor_copy(out=kT_of[g][:, :, kt * P : (kt + 1) * P], in_=kT_ps[:])
 
         PARK = SKV // 2
 
@@ -303,6 +304,10 @@ def tile_groupedqueryattention_pa_kernel(tc, xq, xk_rep, kv, mask, Wv, out):
             g, qt, half = where(n)
             head = PAIR * half + a
             s_ps = psum_s.tile([P, SKV], F32, tag="s")
+            if a == 0 and n < WARM_UP:
+                nc.tensor.matmul(
+                    out=s_ps[:, 0:P], lhsT=ident_f32[:], rhs=ident_f32[:], start=True, stop=True
+                )
             nc.tensor.matmul(
                 out=s_ps[:],
                 lhsT=qT_of[g][:, qt, head, :],
@@ -482,7 +487,7 @@ def tile_groupedqueryattention_pa_kernel(tc, xq, xk_rep, kv, mask, Wv, out):
 
         mask_view = mask_rows.rearrange("(t p) k -> p t k", p=P)
         nc.sync.dma_start(out=mask_sb[:, 0], in_=mask_view[:, 0])
-        load_group(0)
+        load_group(0, [(t, t + 1) for t in range(Q_TILES)])
         nc.sync.dma_start(out=mask_sb[:, 1:], in_=mask_view[:, 1:])
         load_group(1)
         for g in range(PASSES):
@@ -491,14 +496,18 @@ def tile_groupedqueryattention_pa_kernel(tc, xq, xk_rep, kv, mask, Wv, out):
             load_kv(0, t)
         load_group(2)
 
+        zero = const.tile([P, 1], F32)
+        one = const.tile([P, 1], F32)
+        nc.vector.memset(zero[:], 0.0)
+
         with tc.manual_schedule():
+            nc.scalar.activation(out=one[:], in_=zero[:], func=ACT.Exp)
             penalty(0)
             new_group(0)
-            for a in range(GROUP):
-                copy_key_head(0, a, transpose_key_head(0, a))
-                if a == 0:
-                    copy_queries(0, 0, transpose_queries(0, 0))
             copy_penalty(0, transpose_penalty(0))
+            for kt in range(KEY_TILES):
+                copy_key_tile(0, kt, transpose_key_tile(0, kt))
+            copy_queries(0, 0, transpose_queries(0, 0))
 
             def at(stage_of_item, n, *rest):
                 if 0 <= n < N_ITEMS:

@@ -48,6 +48,7 @@ def multiply_step(n):
 
 
 WARM_UP = 10
+VECTOR_SHARE = 4
 WAITING = LAG_MULTIPLY - LAG_QUANTISE + 2
 SUMS = (LAG_MULTIPLY - LAG_EXP) // HALVES + 2
 
@@ -369,7 +370,8 @@ def tile_groupedqueryattention_pa_kernel(tc, xq, xk_rep, kv, mask, Wv, out):
 
         def regroup(n):
             e_grouped = work.tile([P, PAIR * P * PACK], BF16, align_bytes=64)
-            nc.scalar.copy(
+            copy = nc.vector.tensor_copy if n % VECTOR_SHARE == 0 else nc.scalar.copy
+            copy(
                 out=e_grouped[:].bitcast(F32).rearrange("p (a q u) -> p a q u", a=PAIR, u=2),
                 in_=eT_of[n][:].rearrange("p a u q -> p a q u"),
             )
@@ -417,14 +419,34 @@ def tile_groupedqueryattention_pa_kernel(tc, xq, xk_rep, kv, mask, Wv, out):
             ]
             shape = [P, GROUP, OWN, REP]
             o_sb = work.tile(shape, F32)
-            nc.vector.tensor_tensor(
-                out=o_sb[:],
-                in0=own.unsqueeze(3).to_broadcast(shape),
-                in1=inv_sum_of[n // HALVES][:].unsqueeze(2).unsqueeze(3).to_broadcast(shape),
-                op=ALU.mult,
-            )
+            inv_sum = inv_sum_of[n // HALVES][:].unsqueeze(2)
+            if multiply_step(n) >= N_ITEMS:
+                nc.vector.tensor_tensor(
+                    out=o_sb[:],
+                    in0=own.unsqueeze(3).to_broadcast(shape),
+                    in1=inv_sum.unsqueeze(3).to_broadcast(shape),
+                    op=ALU.mult,
+                )
+                store = nc.sync.dma_start
+            else:
+                o_own = work.tile([P, GROUP, OWN], F32)
+                nc.vector.tensor_tensor(
+                    out=o_own[:],
+                    in0=own,
+                    in1=inv_sum.to_broadcast([P, GROUP, OWN]),
+                    op=ALU.mult,
+                )
+                nc.gpsimd.tensor_scalar(
+                    out=o_sb[:],
+                    in0=o_own[:].unsqueeze(3).to_broadcast(shape),
+                    scalar1=1.0,
+                    scalar2=0.0,
+                    op0=ALU.mult,
+                    op1=ALU.add,
+                )
+                store = nc.gpsimd.dma_start
             first = b * SQ + qt * P
-            nc.gpsimd.dma_start(
+            store(
                 out=out_rows[first : first + P, hg * GROUP * P : (hg + 1) * GROUP * P],
                 in_=o_sb[:].rearrange("p h c r -> p (h c r)"),
             )
@@ -504,10 +526,10 @@ def tile_groupedqueryattention_pa_kernel(tc, xq, xk_rep, kv, mask, Wv, out):
             nc.scalar.activation(out=one[:], in_=zero[:], func=ACT.Exp)
             penalty(0)
             new_group(0)
-            copy_penalty(0, transpose_penalty(0))
             for kt in range(KEY_TILES):
                 copy_key_tile(0, kt, transpose_key_tile(0, kt))
             copy_queries(0, 0, transpose_queries(0, 0))
+            copy_penalty(0, transpose_penalty(0))
 
             def at(stage_of_item, n, *rest):
                 if 0 <= n < N_ITEMS:

@@ -370,7 +370,7 @@ def tile_groupedqueryattention_pa_kernel(tc, xq, xk_rep, kv, mask, Wv, out):
 
         def regroup(n):
             e_grouped = work.tile([P, PAIR * P * PACK], BF16, align_bytes=64)
-            copy = nc.vector.tensor_copy if n % VECTOR_SHARE == 0 else nc.scalar.copy
+            copy = nc.vector.tensor_copy if n % VECTOR_SHARE == 2 else nc.scalar.copy
             copy(
                 out=e_grouped[:].bitcast(F32).rearrange("p (a q u) -> p a q u", a=PAIR, u=2),
                 in_=eT_of[n][:].rearrange("p a u q -> p a q u"),

from contextlib import ExitStack

import concourse.mybir as mybir
from concourse.masks import make_identity

F32 = mybir.dt.float32
BF16 = mybir.dt.bfloat16
U32 = mybir.dt.uint32
U8 = mybir.dt.uint8
FP8X4 = mybir.dt.float8_e4m3fn_x4
ALU = mybir.AluOpType
ACT = mybir.ActivationFunctionType

P = 128
PACK = 4
K_PASS = P * PACK

B, SQ, SKV, DIN, HEADS, DIMS = 2, 512, 512, 2048, 16, 2048
HEAD_DIM = DIMS // HEADS
XV = 512
REP = 4
OWN = HEAD_DIM // REP
GROUP = P // OWN
Q_TILES = SQ // P
KEY_TILES = SKV // P
PASSES = DIN // K_PASS
SCALE = HEAD_DIM ** -0.5

PAIR = 2
HALVES = GROUP // PAIR
GROUPS = B * HEADS // GROUP
ITEMS_OF_GROUP = Q_TILES * HALVES
N_ITEMS = GROUPS * ITEMS_OF_GROUP
LAG_MAX = 1
LAG_EXP = 3
LAG_TRANSPOSE = 4
LAG_REGROUP = 5
LAG_QUANTISE = 6
LAG_MULTIPLY = 17
LAG_MULTIPLY_LAST = LAG_QUANTISE + 1


def multiply_step(n):
    if n < N_ITEMS // 2:
        return n + LAG_MULTIPLY
    first = N_ITEMS // 2 + LAG_MULTIPLY
    return max(first + (n - N_ITEMS // 2) // 2, n + LAG_MULTIPLY_LAST)


WARM_UP = 10
VECTOR_SHARE = 4
WAITING = LAG_MULTIPLY - LAG_QUANTISE + 2
SUMS = (LAG_MULTIPLY - LAG_EXP) // HALVES + 2

FLOPS = 2 * B * SKV * DIN * XV + 2 * 2 * B * HEADS * SQ * SKV * HEAD_DIM


def tile_groupedqueryattention_pa_kernel(tc, xq, xk_rep, kv, mask, Wv, out):
    nc = tc.nc
    xq_rows = xq.flatten_outer_dims()
    xk_rows = xk_rep.flatten_outer_dims()
    out_rows = out.flatten_outer_dims()
    mask_rows = mask.rearrange("a b q k -> (a b q) k")
    kv_view = kv.flatten_outer_dims().rearrange("(b u p i) c -> b u i p c", b=B, u=2, i=2)
    wv_view = Wv.rearrange("(g u p i) c -> g p u (i c)", g=PASSES, u=2, p=P, i=2)

    with ExitStack() as ctx:
        const = ctx.enter_context(tc.tile_pool(name="const", bufs=1))
        raw = ctx.enter_context(tc.tile_pool(name="raw", bufs=4))
        stage = ctx.enter_context(tc.tile_pool(name="stage", bufs=2))
        keep = ctx.enter_context(tc.tile_pool(name="keep", bufs=1))
        work = ctx.enter_context(tc.tile_pool(name="work", bufs=4))
        psum_s = ctx.enter_context(tc.psum_pool(name="psum_s", bufs=4))
        psum_t = ctx.enter_context(tc.psum_pool(name="psum_t", bufs=3))
        psum_o = ctx.enter_context(tc.psum_pool(name="psum_o", bufs=1))

        ident_bf = const.tile([P, P], BF16)
        make_identity(nc, ident_bf[:])
        ident_f32 = const.tile([P, P], F32)
        make_identity(nc, ident_f32[:])

        xk_raw, xq_raw, kv_raw = {}, {}, {}

        def rows_of_group(rows, g):
            b, hg = divmod(g, HEADS // GROUP)
            cols = slice(hg * GROUP * P, (hg + 1) * GROUP * P)
            return rows[b * SQ : (b + 1) * SQ, cols].rearrange("(t p) c -> p t c", p=P)

        def load_group(g, pieces=((0, Q_TILES),)):
            xk_sb = raw.tile([P, KEY_TILES, GROUP * P], BF16, bufs=3)
            xq_sb = raw.tile([P, Q_TILES, GROUP * P], BF16, bufs=3)
            for tile_sb, rows in ((xk_sb, xk_rows), (xq_sb, xq_rows)):
                view = rows_of_group(rows, g)
                for lo, hi in pieces:
                    nc.sync.dma_start(out=tile_sb[:, lo:hi], in_=view[:, lo:hi])
            xk_raw[g] = xk_sb
            xq_raw[g] = xq_sb

        def load_kv(b, t):
            kv_sb = raw.tile([P, DIN], BF16)
            nc.sync.dma_start(out=kv_sb[:], in_=kv_view[b, t // 2, t % 2])
            kv_raw[(b, t)] = kv_sb

        mask_sb = const.tile([P, Q_TILES, SKV], BF16)
        neg_penT = const.tile([P, Q_TILES, KEY_TILES, P], F32)

        pen_of = {}

        def penalty(qt):
            pen = work.tile([P, SKV], F32, bufs=2)
            pen_of[qt] = pen
            nc.vector.reciprocal(out=pen[:], in_=mask_sb[:, qt, :])
            nc.vector.tensor_scalar(
                out=pen[:],
                in0=pen[:],
                scalar1=-1.0,
                scalar2=-1.0 / SCALE,
                op0=ALU.add,
                op1=ALU.mult,
            )

        def transpose_penalty(qt):
            penT_ps = psum_t.tile([P, KEY_TILES, P], F32, tag="t")
            for kt in range(KEY_TILES):
                nc.tensor.transpose(
                    penT_ps[:, kt, :], pen_of[qt][:, kt * P : (kt + 1) * P], ident_f32[:]
                )
            return penT_ps

        def copy_penalty(qt, penT_ps):
            nc.scalar.copy(out=neg_penT[:, qt], in_=penT_ps[:])

        qT_of, kT_of = {}, {}

        def new_group(g):
            kT_of[g] = work.tile([P, GROUP, SKV], BF16, name="kT", bufs=2)
            qT_of[g] = work.tile([P, Q_TILES, GROUP, P], BF16, name="qT", bufs=2)

        def transpose_key_tile(g, kt):
            kT_ps = psum_t.tile([P, GROUP, P], BF16, tag="t")
            for a in range(GROUP):
                nc.tensor.transpose(
                    kT_ps[:, a, :], xk_raw[g][:, kt, a * P : (a + 1) * P], ident_bf[:]
                )
            return kT_ps

        def copy_key_tile(g, kt, kT_ps):
            nc.vector.tensor_copy(out=kT_of[g][:, :, kt * P : (kt + 1) * P], in_=kT_ps[:])

        PARK = SKV // 2

        def parked(g):
            return out_rows[B * SQ - P : B * SQ, g * PARK : (g + 1) * PARK]

        def transpose_keys(g):
            kc_ps = psum_t.tile([P, KEY_TILES, P], BF16, tag="t")
            for kt in range(KEY_TILES):
                different = xk_raw[g][:, kt, :].rearrange("p (c r) -> p c r", r=REP)[:, :, 0]
                nc.tensor.transpose(kc_ps[:, kt, :], different, ident_bf[:])
            return kc_ps

        def spread_keys(g, kc_ps):
            new_group(g)
            kc_sb = work.tile([P, SKV], BF16, bufs=2)
            nc.scalar.copy(out=kc_sb[:], in_=kc_ps[:].rearrange("p t r -> p (t r)"))
            nc.sync.dma_start(out=parked(g), in_=kc_sb[:].bitcast(F32))
            kT_words = kT_of[g][:].bitcast(F32)
            for r in range(REP):
                nc.sync.dma_start(
                    out=kT_words[r:P:REP, :, :], in_=parked(g).rearrange("(a j) w -> j a w", a=GROUP)
                )

        def transpose_queries(g, qt):
            qT_ps = psum_t.tile([P, GROUP, P], BF16, tag="t")
            for a in range(GROUP):
                nc.tensor.transpose(
                    qT_ps[:, a, :], xq_raw[g][:, qt, a * P : (a + 1) * P], ident_bf[:]
                )
            return qT_ps

        def multiply_queries(g, qt):
            qT_ps = psum_t.tile([P, GROUP, P], BF16, tag="t")
            for a in range(GROUP):
                nc.tensor.matmul(
                    out=qT_ps[:, a, :],
                    lhsT=xq_raw[g][:, qt, a * P : (a + 1) * P],
                    rhs=ident_bf[:],
                    start=True,
                    stop=True,
                )
            return qT_ps

        def copy_queries(g, qt, qT_ps):
            nc.scalar.copy(out=qT_of[g][:, qt], in_=qT_ps[:])

        wv_raw = const.tile([P, PASSES, 2, 2 * XV], BF16)
        wv_codes = const.tile([P, PASSES, XV], U32, align_bytes=64)
        wv_scales = const.tile([P, PASSES, XV], U8, align_bytes=64)

        def group_wv(g):
            wv_grouped = stage.tile([P, XV, PACK], BF16, align_bytes=64)
            nc.gpsimd.tensor_scalar(
                out=wv_grouped[:],
                in0=wv_raw[:, g].rearrange("p u (i c) -> p c (u i)", i=2),
                scalar1=1.0,
                scalar2=0.0,
                op0=ALU.mult,
                op1=ALU.add,
            )
            return wv_grouped

        def quantise_wv(g, wv_grouped):
            nc.vector.quantize_mx(
                out=wv_codes[:, g, :].bitcast(FP8X4),
                scales=wv_scales[:, g, :],
                in_=wv_grouped[:].rearrange("p c t -> p (c t)"),
            )

        kv_grouped_of, kv_codes_of, v_grouped_of, values = {}, {}, {}, {}

        def transpose_kv(b, t, half):
            kv_words = kv_raw[(b, t)][:].bitcast(F32)
            kvT_ps = psum_t.tile([P, 2, 2, P], F32, tag="t")
            for a in range(2):
                for u in range(2):
                    w0 = (2 * half + a) * (K_PASS // 2) + u * P
                    nc.tensor.transpose(
                        kvT_ps[:, a, u, :], kv_words[:, w0 : w0 + P], ident_f32[:]
                    )
            return kvT_ps

        def copy_kv(b, t, half, kvT_ps):
            if half == 0:
                kv_grouped_of[(b, t)] = stage.tile(
                    [P, PASSES * P * PACK], BF16, name="kv_grouped", align_bytes=64
                )
            grouped_words = (
                kv_grouped_of[(b, t)][:]
                .bitcast(F32)
                .rearrange("p (g r u) -> p g r u", g=PASSES, r=P)
            )
            nc.scalar.copy(
                out=grouped_words[:, 2 * half : 2 * half + 2, :, :],
                in_=kvT_ps[:].rearrange("p a u r -> p a r u"),
            )

        def quantise_kv(b, t):
            if t == 0:
                kv_codes = keep.tile([P, KEY_TILES, PASSES, P], U32, align_bytes=64)
                kv_scales = keep.tile([P, KEY_TILES, PASSES, P], U8, align_bytes=64)
                kv_codes_of[b] = (kv_codes, kv_scales)
            kv_codes, kv_scales = kv_codes_of[b]
            nc.vector.quantize_mx(
                out=kv_codes[:, t].rearrange("p g r -> p (g r)").bitcast(FP8X4),
                scales=kv_scales[:, t].rearrange("p g r -> p (g r)"),
                in_=kv_grouped_of[(b, t)][:],
            )

        def project(b, j):
            kv_codes, kv_scales = kv_codes_of[b]
            cols = slice(j * P, (j + 1) * P)
            xv_ps = psum_s.tile([P, KEY_TILES, P], F32, tag="s")
            for t in range(KEY_TILES):
                for g in range(PASSES):
                    nc.tensor.matmul_mx(
                        out=xv_ps[:, t, :],
                        lhsT=kv_codes[:, t, g, :].bitcast(FP8X4),
                        lhsT_scale=kv_scales[:, t, g, :],
                        rhs=wv_codes[:, g, cols].bitcast(FP8X4),
                        rhs_scale=wv_scales[:, g, cols],
                        start=(g == 0),
                        stop=(g == PASSES - 1),
                    )
            return xv_ps

        def copy_xv(b, j, xv_ps):
            if j == 0:
                v_grouped_of[b] = stage.tile(
                    [P, XV, PACK], BF16, name="v_grouped", align_bytes=64, bufs=1
                )
            nc.scalar.copy(
                out=v_grouped_of[b][:, j * P : (j + 1) * P, :],
                in_=xv_ps[:].rearrange("p t f -> p f t"),
            )

        def quantise_v(b):
            v_codes = keep.tile([P, XV], U32, align_bytes=64, bufs=B)
            v_scales = keep.tile([P, XV], U8, align_bytes=64, bufs=B)
            nc.vector.quantize_mx(
                out=v_codes[:].bitcast(FP8X4),
                scales=v_scales[:],
                in_=v_grouped_of[b][:].rearrange("p f t -> p (f t)"),
            )
            values[b] = (v_codes, v_scales)

        banks_of, neg_s_of, shift_of, e_of, eT_of, grouped_of, codes_of = {}, {}, {}, {}, {}, {}, {}
        sum_of, inv_sum_of, o_of = {}, {}, {}

        def where(n):
            g, rest = divmod(n, ITEMS_OF_GROUP)
            qt, half = divmod(rest, HALVES)
            return g, qt, half

        def scores(n, a):
            g, qt, half = where(n)
            head = PAIR * half + a
            s_ps = psum_s.tile([P, SKV], F32, tag="s")
            if a == 0 and n < WARM_UP:
                nc.tensor.matmul(
                    out=s_ps[:, 0:P], lhsT=ident_f32[:], rhs=ident_f32[:], start=True, stop=True
                )
            nc.tensor.matmul(
                out=s_ps[:],
                lhsT=qT_of[g][:, qt, head, :],
                rhs=kT_of[g][:, head, :],
                start=True,
                stop=False,
            )
            banks_of[(n, a)] = s_ps

        def add_penalty(n, a):
            g, qt, half = where(n)
            for kt in range(KEY_TILES):
                nc.tensor.matmul(
                    out=banks_of[(n, a)][:, kt * P : (kt + 1) * P],
                    lhsT=neg_penT[:, qt, kt, :],
                    rhs=ident_f32[:],
                    is_transpose=True,
                    start=False,
                    stop=(kt == KEY_TILES - 1),
                )

        def maximum(n, a):
            if a == 0:
                neg_s_of[n] = work.tile([P, PAIR, SKV], F32, name="neg_s")
                shift_of[n] = work.tile([P, PAIR], F32, name="shift")
            nc.vector.tensor_scalar(
                out=neg_s_of[n][:, a, :],
                in0=banks_of[(n, a)][:],
                scalar1=-SCALE,
                scalar2=None,
                op0=ALU.mult,
                op1=ALU.min,
                accum_out=shift_of[n][:, a : a + 1],
            )

        def exponential(n, a):
            if a == 0:
                e_of[n] = work.tile([P, PAIR, SKV], BF16, name="e_sb")
                if n % HALVES == 0:
                    sum_of[n // HALVES] = work.tile([P, GROUP], F32, name="row_sum", bufs=SUMS)
            col = PAIR * (n % HALVES) + a
            nc.scalar.activation(
                out=e_of[n][:, a, :],
                in_=neg_s_of[n][:, a, :],
                func=ACT.Exp,
                bias=shift_of[n][:, a : a + 1],
                scale=-1.0,
                accum_out=sum_of[n // HALVES][:, col : col + 1],
            )

        def transposes(n):
            eT_ps = psum_t.tile([P, PAIR, 2, P], F32, tag="t")
            e_words = e_of[n][:].rearrange("p a k -> p (a k)").bitcast(F32)
            for a in range(PAIR):
                for u in range(2):
                    w0 = (2 * a + u) * P
                    nc.tensor.transpose(eT_ps[:, a, u, :], e_words[:, w0 : w0 + P], ident_f32[:])
            eT_of[n] = eT_ps

        def regroup(n):
            e_grouped = work.tile([P, PAIR * P * PACK], BF16, align_bytes=64)
            copy = nc.vector.tensor_copy if n % VECTOR_SHARE == 2 else nc.scalar.copy
            copy(
                out=e_grouped[:].bitcast(F32).rearrange("p (a q u) -> p a q u", a=PAIR, u=2),
                in_=eT_of[n][:].rearrange("p a u q -> p a q u"),
            )
            grouped_of[n] = e_grouped

        def quantise(n):
            e_codes = work.tile([P, PAIR * P], U32, align_bytes=64, bufs=WAITING)
            e_scales = work.tile([P, PAIR * P], U8, align_bytes=64, bufs=WAITING)
            nc.vector.quantize_mx(
                out=e_codes[:].bitcast(FP8X4), scales=e_scales[:], in_=grouped_of[n][:]
            )
            codes_of[n] = (e_codes, e_scales)

        def multiply(n):
            g, qt, half = where(n)
            b, hg = divmod(g, HEADS // GROUP)
            v_codes, v_scales = values[b]
            e_codes, e_scales = codes_of[n]
            group_cols = slice(hg * P, (hg + 1) * P)
            if half == 0:
                o_of[n // HALVES] = psum_o.tile([P, GROUP, GROUP * OWN], F32, name="o_ps")
            for a in range(PAIR):
                queries = slice(a * P, (a + 1) * P)
                nc.tensor.matmul_mx(
                    out=o_of[n // HALVES][:, PAIR * half + a, :],
                    lhsT=e_codes[:, queries].bitcast(FP8X4),
                    lhsT_scale=e_scales[:, queries],
                    rhs=v_codes[:, group_cols].bitcast(FP8X4),
                    rhs_scale=v_scales[:, group_cols],
                    start=True,
                    stop=True,
                )
            if half == HALVES - 1:
                inv_sum = work.tile([P, GROUP], F32)
                nc.vector.reciprocal(out=inv_sum[:], in_=sum_of[n // HALVES][:])
                inv_sum_of[n // HALVES] = inv_sum

        def finish(n):
            if n % HALVES != HALVES - 1:
                return
            g, qt, half = where(n)
            b, hg = divmod(g, HEADS // GROUP)
            own = o_of[n // HALVES][:].rearrange("p h (g c) -> p (h g) c", c=OWN)[
                :, 0 : GROUP * GROUP : GROUP + 1, :
            ]
            shape = [P, GROUP, OWN, REP]
            o_sb = work.tile(shape, F32)
            inv_sum = inv_sum_of[n // HALVES][:].unsqueeze(2)
            if multiply_step(n) >= N_ITEMS:
                nc.vector.tensor_tensor(
                    out=o_sb[:],
                    in0=own.unsqueeze(3).to_broadcast(shape),
                    in1=inv_sum.unsqueeze(3).to_broadcast(shape),
                    op=ALU.mult,
                )
                store = nc.sync.dma_start
            else:
                o_own = work.tile([P, GROUP, OWN], F32)
                nc.vector.tensor_tensor(
                    out=o_own[:],
                    in0=own,
                    in1=inv_sum.to_broadcast([P, GROUP, OWN]),
                    op=ALU.mult,
                )
                nc.gpsimd.tensor_scalar(
                    out=o_sb[:],
                    in0=o_own[:].unsqueeze(3).to_broadcast(shape),
                    scalar1=1.0,
                    scalar2=0.0,
                    op0=ALU.mult,
                    op1=ALU.add,
                )
                store = nc.gpsimd.dma_start
            first = b * SQ + qt * P
            store(
                out=out_rows[first : first + P, hg * GROUP * P : (hg + 1) * GROUP * P],
                in_=o_sb[:].rearrange("p h c r -> p (h c r)"),
            )

        with_scores, copies, starts, late_copies = {}, {}, {}, {}

        def at_step(place, k, chore):
            place.setdefault(k, []).append(chore)

        def in_two_steps(k, first, second, key):
            made = {}
            at_step(starts, k, lambda: made.update(x=first(*key)))
            at_step(copies, k + 1, lambda: second(*key, made["x"]))

        def in_one_step(k, first, second, key):
            made = {}
            at_step(with_scores, k, lambda: made.update(x=first(*key)))
            at_step(late_copies, k, lambda: second(*key, made["x"]))

        BY_MATMUL = N_ITEMS // 2

        def prepare_queries(k, g, qt):
            if k < BY_MATMUL:
                in_one_step(k, multiply_queries, copy_queries, (g, qt))
            else:
                in_two_steps(k, transpose_queries, copy_queries, (g, qt))

        for qt in range(1, Q_TILES):
            at_step(starts, HALVES * (qt - 1), lambda qt=qt: penalty(qt))
            in_two_steps(HALVES * (qt - 1), transpose_penalty, copy_penalty, (qt,))
            prepare_queries(qt - 1, 0, qt)
        for g in range(1, GROUPS):
            before = ITEMS_OF_GROUP * (g - 1)
            in_two_steps(before, transpose_keys, spread_keys, (g,))
            for qt in range(Q_TILES):
                prepare_queries(before + 2 * qt + 1, g, qt)
            if g + 1 < GROUPS and g > 1:
                at_step(starts, before, lambda g=g: load_group(g + 1))
        VALUES_0 = 3
        VALUES_1 = 17
        for c in range(2 * KEY_TILES):
            t, half = divmod(c, 2)
            in_two_steps(VALUES_0 + c, transpose_kv, copy_kv, (0, t, half))
            in_two_steps(VALUES_1 + 2 * c, transpose_kv, copy_kv, (1, t, half))
            if half == 1:
                at_step(starts, VALUES_0 + c + 1, lambda t=t: quantise_kv(0, t))
                at_step(starts, VALUES_0 + c + 1, lambda t=t: load_kv(1, t))
                at_step(starts, VALUES_1 + 2 * c + 1, lambda t=t: quantise_kv(1, t))
        for g in range(PASSES):
            in_two_steps(1 + g, group_wv, quantise_wv, (g,))
        PROJECT_0 = VALUES_0 + 2 * KEY_TILES + 1
        PROJECT_1 = VALUES_1 + 4 * KEY_TILES + 1
        for j in range(XV // P):
            made_0, made_1 = {}, {}
            for b, k, made in ((0, PROJECT_0 + j, made_0), (1, PROJECT_1 + 2 * j, made_1)):
                at_step(with_scores, k, lambda b=b, j=j, made=made: made.update(x=project(b, j)))
                at_step(copies, k + 1, lambda b=b, j=j, made=made: copy_xv(b, j, made["x"]))
        at_step(starts, PROJECT_0 + XV // P, lambda: quantise_v(0))
        at_step(starts, PROJECT_1 + 2 * (XV // P) - 1, lambda: quantise_v(1))

        mask_view = mask_rows.rearrange("(t p) k -> p t k", p=P)
        nc.sync.dma_start(out=mask_sb[:, 0], in_=mask_view[:, 0])
        load_group(0, [(t, t + 1) for t in range(Q_TILES)])
        nc.sync.dma_start(out=mask_sb[:, 1:], in_=mask_view[:, 1:])
        load_group(1)
        for g in range(PASSES):
            nc.sync.dma_start(out=wv_raw[:, g], in_=wv_view[g])
        for t in range(KEY_TILES):
            load_kv(0, t)
        load_group(2)

        zero = const.tile([P, 1], F32)
        one = const.tile([P, 1], F32)
        nc.vector.memset(zero[:], 0.0)

        with tc.manual_schedule():
            nc.scalar.activation(out=one[:], in_=zero[:], func=ACT.Exp)
            penalty(0)
            new_group(0)
            for kt in range(KEY_TILES):
                copy_key_tile(0, kt, transpose_key_tile(0, kt))
            copy_queries(0, 0, transpose_queries(0, 0))
            copy_penalty(0, transpose_penalty(0))

            def at(stage_of_item, n, *rest):
                if 0 <= n < N_ITEMS:
                    stage_of_item(n, *rest)

            multiplies = {}
            for n in range(N_ITEMS):
                multiplies.setdefault(multiply_step(n), []).append(n)
            for k in range(multiply_step(N_ITEMS - 1) + 2):
                for n in multiplies.get(k - 1, []):
                    finish(n)
                at(regroup, k - LAG_REGROUP)
                at(maximum, k - LAG_MAX, 0)
                at(transposes, k - LAG_TRANSPOSE)
                at(quantise, k - LAG_QUANTISE)
                at(maximum, k - LAG_MAX, 1)
                for chore in with_scores.get(k, []):
                    chore()
                at(scores, k, 0)
                for n in multiplies.get(k, []):
                    multiply(n)
                at(scores, k, 1)
                at(add_penalty, k, 0)
                at(add_penalty, k, 1)
                at(exponential, k - LAG_EXP, 0)
                at(exponential, k - LAG_EXP, 1)
                for place in (copies, starts, late_copies):
                    for chore in place.get(k, []):
                        chore()
